import numpy as np
import ml_dtypes


def mxq(x, axis, fmt="e4m3"):
    dtype, down = {"e4m3": (ml_dtypes.float8_e4m3fn, 7), "e5m2": (ml_dtypes.float8_e5m2, 14)}[fmt]
    v = np.moveaxis(np.asarray(x, np.float32).astype(ml_dtypes.bfloat16).astype(np.float64), axis, -1)
    blocks = v.reshape(v.shape[:-1] + (-1, 32))
    amax = np.abs(blocks).max(-1, keepdims=True)
    byte = np.maximum(np.where(amax > 0, np.frexp(amax)[1] - 1 + 127, 0) - down, 1)
    scale = np.exp2(byte - 127.0)
    codes = (blocks / scale).astype(np.float32).astype(dtype).astype(np.float64)
    return np.moveaxis((codes * scale).reshape(v.shape), -1, axis)


WIDE = False


def mx_kscale(k):
    if not WIDE:
        return np.ones(k)
    levels = np.array([10, -10, 5, -5, 0])
    a = np.random.permutation(np.resize(levels, k // 512 * 4)).reshape(k // 512, 4)
    idx = np.arange(k)
    return np.exp2(a[idx // 512, idx % 128 // 32])


BF16 = ml_dtypes.bfloat16


def bf(x):
    return np.asarray(x, np.float32).astype(BF16)


def f64(x):
    return np.asarray(x).astype(np.float64)


E2M1 = np.array([0.0, 0.5, 1.0, 1.5, 2.0, 3.0, 4.0, 6.0, -0.0, -0.5, -1.0, -1.5, -2.0, -3.0, -4.0, -6.0])


def pack_weight(w, fmt):
    k, n = w.shape
    w = f64(bf(w)).reshape(k // 32, 32, n)
    amax = np.abs(w).max(1)
    if fmt == "e4m3":
        byte = np.frexp(amax)[1] - 1 + 127 - 7
    else:
        mant, ex = np.frexp(amax / 6.0)
        byte = np.where(mant > 0.5, ex, ex - 1) + 127
    byte = np.clip(np.where(amax > 0, byte, 1), 1, 254)
    scaled = (w * np.exp2(127.0 - byte)[:, None, :]).reshape(k, n).astype(np.float32)
    by_word = np.ascontiguousarray(scaled.reshape(k // 512, 128, 4, n).transpose(0, 1, 3, 2))
    if fmt == "e4m3":
        words = by_word.astype(ml_dtypes.float8_e4m3fn).view(np.uint8)
    else:
        c = by_word.astype(ml_dtypes.float4_e2m1fn).view(np.uint8) & 0xF
        words = c[..., 0::2] | (c[..., 1::2] << 4)
    return np.ascontiguousarray(words), np.ascontiguousarray(byte.astype(np.uint8).reshape(k // 512, 16, n))


def unpack_weight(words, scales, fmt):
    g, p, n, _ = words.shape
    if fmt == "e4m3":
        vals = np.ascontiguousarray(words).view(ml_dtypes.float8_e4m3fn).astype(np.float64)
    else:
        nib = np.empty((g, p, n, 4), np.uint8)
        nib[..., 0::2] = words & 0xF
        nib[..., 1::2] = words >> 4
        vals = E2M1[nib]
    vals = vals * np.repeat(np.exp2(scales.astype(np.float64) - 127.0), 8, axis=1)[..., None]
    return vals.transpose(0, 1, 3, 2).reshape(g * 512, n)

def pack4(w):
    words, scales = pack_weight(w, "e2m1")
    return words.reshape(words.shape[0], 128, -1), scales


def unpack4(words, scales):
    return unpack_weight(words.reshape(words.shape[0], 128, -1, 2), scales, "e2m1")


B, C, H, W = 128, 1024, 3, 3
C3, CH, P = 3 * C, C // 2, H * W


def sigmoid(v):
    return 1.0 / (1.0 + np.exp(-v))


def setup_inputs():
    s, t = mx_kscale(C3), mx_kscale(CH)
    n = np.random.standard_normal
    fv = bf(n((B, C3, H, W)) * s[None, :, None, None])
    ft = bf(n((B, C)))
    wa = n((CH, C3)) / np.sqrt(C3) / s[None, :] * t[:, None]
    ba = bf(n(CH) * 0.3 * t)
    wb = n((C, CH)) * 2.0 / np.sqrt(CH) / t[None, :]
    bb = bf(n(C) * 0.5)
    Wfc2 = bf(n((C, C)) / np.sqrt(C))
    bfc2 = bf(n(C) * 0.3)
    Wa_words, Wa_scales = pack4(np.ascontiguousarray(wa.T))
    Wb_words, Wb_scales = pack4(np.ascontiguousarray(wb.T))
    return {
        "fv": fv,
        "ft": ft,
        "Wa_words": Wa_words,
        "Wa_scales": Wa_scales,
        "ba": ba,
        "Wb_words": Wb_words,
        "Wb_scales": Wb_scales,
        "bb": bb,
        "Wfc2": Wfc2,
        "bfc2": bfc2,
    }


def reference(fv, ft, Wa_words, Wa_scales, ba, Wb_words, Wb_scales, bb, Wfc2, bfc2):
    h = np.maximum((unpack4(Wa_words, Wa_scales).T @ mxq(f64(fv).reshape(B, C3, P), 1, "e4m3")) + f64(ba)[None, :, None], 0.0)
    fv2 = (unpack4(Wb_words, Wb_scales).T @ mxq(h, 1, "e4m3")) + f64(bb)[None, :, None]
    gate = sigmoid(fv2.mean(axis=2))
    ft2 = f64(ft) @ f64(Wfc2).T + f64(bfc2)
    return ft2 + ft2 * gate

@@ -1,0 +1,287 @@
+from contextlib import ExitStack
+
+import concourse.mybir as mybir
+from concourse.masks import make_identity
+
+F32 = mybir.dt.float32
+BF16 = mybir.dt.bfloat16
+I32 = mybir.dt.int32
+U32 = mybir.dt.uint32
+U8 = mybir.dt.uint8
+FP8X4 = mybir.dt.float8_e4m3fn_x4
+FP4X4 = mybir.dt.float4_e2m1fn_x4
+ADD = mybir.AluOpType.add
+MULT = mybir.AluOpType.mult
+FUNC = mybir.ActivationFunctionType
+
+P = 128
+PACK = 4
+K_PASS = P * PACK
+C_IN = 3072
+HID = 512
+C_OUT = 1024
+PIX = 9
+CHUNKS = C_IN // K_PASS
+BANK = 512
+HALVES = C_OUT // BANK
+PAIR = 2
+FLIP_BANKS = 3
+SUM_BANKS = 8 - FLIP_BANKS
+K_FC = C_OUT // (2 * P)
+W_TILES = BANK // P
+
+FLOPS = 2 * P * PIX * (C_IN * HID + HID * C_OUT) + 2 * P * C_OUT * C_OUT
+
+
+def pixel_runs(first, count, step):
+    return [(x, min(step, first + count - x)) for x in range(first, first + count, step)]
+
+
+def tile_joint_module_pb_kernel(tc, fv, ft, Wa_words, Wa_scales, ba, Wb_words, Wb_scales, bb, Wfc2, bfc2, out):
+    nc = tc.nc
+    with ExitStack() as ctx:
+        ctx.enter_context(tc.manual_schedule())
+        keep = ctx.enter_context(tc.tile_pool(name="keep", bufs=1))
+        stream = ctx.enter_context(tc.tile_pool(name="stream", bufs=2))
+        flip_banks = ctx.enter_context(tc.psum_pool(name="flip_banks", bufs=FLIP_BANKS))
+        sum_banks = ctx.enter_context(tc.psum_pool(name="sum_banks", bufs=SUM_BANKS))
+
+        bias_rows = keep.tile([P, HID + 2 * C_OUT], BF16)
+        nc.vector.memset(bias_rows[:].bitcast(I32), 0)
+        bb_at = HID
+        bfc2_at = HID + C_OUT
+        nc.scalar.dma_start(out=bias_rows[0:1, 0:HID], in_=ba.rearrange("(o n) -> o n", o=1))
+        nc.scalar.dma_start(out=bias_rows[0:1, bb_at : bb_at + C_OUT], in_=bb.rearrange("(o n) -> o n", o=1))
+        nc.scalar.dma_start(out=bias_rows[0:1, bfc2_at : bfc2_at + C_OUT], in_=bfc2.rearrange("(o n) -> o n", o=1))
+        ident = keep.tile([P, P], F32)
+        make_identity(nc, ident[:])
+        ones = keep.tile([P, P], BF16)
+        nc.vector.memset(ones[:], 1.0)
+        warm = keep.tile([P, 1], F32)
+        nc.vector.memset(warm[:], 0.0)
+        nc.scalar.activation(out=warm[:], in_=warm[:], func=FUNC.Sigmoid)
+
+        wa_planes = keep.tile([P, CHUNKS, HID], U8, align_bytes=64)
+        wb_planes = keep.tile([P, C_OUT], U8, align_bytes=64)
+        nc.vector.memset(wa_planes[:].rearrange("p g n -> p (g n)").bitcast(I32), 0)
+        nc.vector.memset(wb_planes[:].bitcast(I32), 0)
+
+        fv_rows = fv.rearrange("b c i j -> b (c i j)")
+        row = K_PASS * PIX
+        raw = [keep.tile([P, row], BF16, name="raw%d" % g) for g in range(CHUNKS)]
+        wa_words = keep.tile([P, CHUNKS, 2 * HID], U8, align_bytes=64)
+        wb_words = keep.tile([P, 2 * C_OUT], U8, align_bytes=64)
+        ft_sb = keep.tile([P, C_OUT], BF16)
+        w_sb = keep.tile([P, HALVES * W_TILES, C_OUT], BF16)
+
+        def load_chunk(g):
+            nc.sync.dma_start(out=raw[g][:], in_=fv_rows[:, g * row : (g + 1) * row])
+
+        load_chunk(0)
+        load_chunk(1)
+        for quad in range(4):
+            nc.sync.dma_start(
+                out=wa_planes[32 * quad : 32 * quad + 4].bitcast(I32),
+                in_=Wa_scales.bitcast(I32)[:, 4 * quad : 4 * quad + 4, :].rearrange("g r n -> r g n"),
+            )
+        nc.sync.dma_start(out=wa_words[:].bitcast(I32), in_=Wa_words.bitcast(I32).rearrange("g p n -> p g n"))
+        for g in range(2, CHUNKS):
+            load_chunk(g)
+        nc.sync.dma_start(out=ft_sb[:], in_=ft)
+        w_rows = Wfc2.rearrange("(a r) c -> r a c", r=P)
+        for half in range(HALVES):
+            a_range = slice(half * W_TILES, (half + 1) * W_TILES)
+            nc.sync.dma_start(out=w_sb[:, a_range, :], in_=w_rows[:, a_range, :])
+        for quad in range(4):
+            nc.sync.dma_start(
+                out=wb_planes[32 * quad : 32 * quad + 4].bitcast(I32),
+                in_=Wb_scales.bitcast(I32)[0, 4 * quad : 4 * quad + 4, :],
+            )
+        nc.sync.dma_start(out=wb_words[:].bitcast(I32), in_=Wb_words.bitcast(I32)[0])
+
+        ba_all = keep.tile([P, HID], F32)
+        bb_all = keep.tile([P, C_OUT], F32)
+        spread = sum_banks.tile([P, BANK], F32, tag="sum")
+        nc.tensor.matmul(out=spread[:], lhsT=ones[:], rhs=bias_rows[:, 0:HID], start=True, stop=True)
+        nc.scalar.copy(out=ba_all[:], in_=spread[:])
+        for half in range(HALVES):
+            spread = sum_banks.tile([P, BANK], F32, tag="sum")
+            nc.tensor.matmul(
+                out=spread[:], lhsT=ones[:], rhs=bias_rows[:, bb_at + half * BANK : bb_at + (half + 1) * BANK],
+                start=True, stop=True,
+            )
+            nc.scalar.copy(out=bb_all[:, half * BANK : (half + 1) * BANK], in_=spread[:])
+
+        def flip_and_quantise(sorted_tile, n, relu, codes, scales):
+            bank = flip_banks.tile([P, PAIR, 2, P], F32, tag="flip")
+            for x in range(n):
+                for u in range(2):
+                    words = sorted_tile[:, x, u].rearrange("b p e -> b (p e)").bitcast(F32)
+                    nc.tensor.transpose(out=bank[:, x, u, :], in_=words, identity=ident[:])
+            grouped = stream.tile([P, PAIR, P, PACK], BF16, tag="grouped", bufs=6, align_bytes=64)
+            if relu:
+                for x in range(n):
+                    nc.vector.tensor_scalar_max(
+                        out=grouped[:, x].rearrange("p b (u e) -> p b u e", u=2),
+                        in0=bank[:, x].bitcast(BF16).rearrange("p u (b e) -> p b u e", e=2),
+                        scalar1=0.0,
+                    )
+            else:
+                nc.scalar.copy(
+                    out=grouped[:, 0:n].rearrange("p x b t -> p (x b t)").bitcast(F32)
+                    .rearrange("p (x b u) -> p x b u", x=n, u=2),
+                    in_=bank[:, 0:n].rearrange("p x u b -> p x b u"),
+                )
+            nc.vector.quantize_mx(
+                out=codes.rearrange("p x b -> p (x b)").bitcast(FP8X4),
+                scales=scales.rearrange("p x b -> p (x b)"),
+                in_=grouped[:, 0:n].rearrange("p x b t -> p (x b t)"),
+            )
+
+        fv_codes = keep.tile([P, CHUNKS, PIX, P], U32, align_bytes=64)
+        fv_scales = keep.tile([P, CHUNKS, PIX, P], U8, align_bytes=64)
+        waves = pixel_runs(0, PIX, SUM_BANKS)
+        steps = [(first, count, g) for first, count in waves for g in range(CHUNKS)]
+        sorted_fv = {}
+        hidden = {}
+
+        def sort_step(i):
+            first, count, g = steps[i]
+            sorted_fv[i] = []
+            for x0, n in pixel_runs(first, count, PAIR):
+                tile_x = stream.tile([P, PAIR, 2, P, 2], BF16, tag="sorted", bufs=6, name="sorted")
+                nc.vector.tensor_copy(
+                    out=tile_x[:, 0:n].rearrange("b x u p e -> b p x u e"),
+                    in_=raw[g][:].rearrange("b (p u e x) -> b p x u e", u=2, e=2, x=PIX)[:, :, x0 : x0 + n],
+                )
+                sorted_fv[i].append((x0, n, tile_x))
+
+        def flip_step(i):
+            g = steps[i][2]
+            for x0, n, tile_x in sorted_fv[i]:
+                flip_and_quantise(tile_x, n, False, fv_codes[:, g, x0 : x0 + n, :], fv_scales[:, g, x0 : x0 + n, :])
+
+        def multiply_step(i):
+            first, count, g = steps[i]
+            for pix in range(first, first + count):
+                if g == 0:
+                    hidden[pix] = sum_banks.tile([P, HID], F32, tag="sum", name="hidden")
+                nc.tensor.matmul_mx(
+                    out=hidden[pix][:],
+                    lhsT=fv_codes[:, g, pix, :].bitcast(FP8X4),
+                    lhsT_scale=fv_scales[:, g, pix, :],
+                    rhs=wa_words[:, g, :].bitcast(FP4X4),
+                    rhs_scale=wa_planes[:, g, :],
+                    start=(g == 0),
+                    stop=(g == CHUNKS - 1),
+                )
+
+        def first_convolution(rounds):
+            for i in rounds:
+                if i + 1 < len(steps):
+                    sort_step(i + 1)
+                if i < len(steps):
+                    flip_step(i)
+                if i >= 1:
+                    multiply_step(i - 1)
+
+        h_codes = keep.tile([P, PIX, P], U32, align_bytes=64)
+        h_scales = keep.tile([P, PIX, P], U8, align_bytes=64)
+
+        def add_bias(first, count):
+            sorted_h = []
+            for x0, n in pixel_runs(first, count, PAIR):
+                tile_x = stream.tile([P, PAIR, 2, P, 2], BF16, tag="sorted_h", bufs=3, name="sorted_h")
+                for x in range(n):
+                    nc.vector.tensor_tensor(
+                        out=tile_x[:, x],
+                        in0=hidden[x0 + x][:].rearrange("b (p u e) -> b u p e", u=2, e=2),
+                        in1=ba_all[:].rearrange("b (p u e) -> b u p e", u=2, e=2),
+                        op=ADD,
+                    )
+                sorted_h.append((x0, n, tile_x))
+            return sorted_h
+
+        def flip_hidden(sorted_h):
+            for x0, n, tile_x in sorted_h:
+                flip_and_quantise(tile_x, n, True, h_codes[:, x0 : x0 + n, :], h_scales[:, x0 : x0 + n, :])
+
+        def second_convolution(first, count, pixel_sum):
+            for pix in range(first, first + count):
+                for half in range(HALVES):
+                    nc.tensor.matmul_mx(
+                        out=pixel_sum[half][:],
+                        lhsT=h_codes[:, pix, :].bitcast(FP8X4),
+                        lhsT_scale=h_scales[:, pix, :],
+                        rhs=wb_words[:, half * 2 * BANK : (half + 1) * 2 * BANK].bitcast(FP4X4),
+                        rhs_scale=wb_planes[:, half * BANK : (half + 1) * BANK],
+                        start=(pix == 0),
+                        stop=(pix == PIX - 1),
+                    )
+
+        ftT = keep.tile([P, K_FC, 2, P], BF16)
+        wT = keep.tile([P, K_FC, C_OUT, 2], BF16)
+        ft2 = keep.tile([P, C_OUT], F32)
+
+        def flip_text_features():
+            bank = flip_banks.tile([P, K_FC, P], F32, tag="flip")
+            for j in range(K_FC):
+                nc.tensor.transpose(out=bank[:, j, :], in_=ft_sb[:].bitcast(F32)[:, j * P : (j + 1) * P], identity=ident[:])
+            nc.scalar.copy(out=ftT[:], in_=bank[:].bitcast(BF16).rearrange("q j (b e) -> q j e b", e=2))
+
+        def plain_layer(half):
+            cols = slice(half * BANK, (half + 1) * BANK)
+            ft2_sum = sum_banks.tile([P, BANK], F32, tag="sum")
+            for j in range(K_FC + 1):
+                if j < K_FC:
+                    bank = flip_banks.tile([P, W_TILES, P], F32, tag="flip")
+                    for a in range(W_TILES):
+                        nc.tensor.transpose(
+                            out=bank[:, a, :],
+                            in_=w_sb[:, half * W_TILES + a, :].bitcast(F32)[:, j * P : (j + 1) * P],
+                            identity=ident[:],
+                        )
+                    nc.scalar.copy(
+                        out=wT[:, j, cols, :].rearrange("q o e -> q (o e)").bitcast(F32),
+                        in_=bank[:].rearrange("q a r -> q (a r)"),
+                    )
+                if j >= 1:
+                    for e in range(2):
+                        nc.tensor.matmul(
+                            out=ft2_sum[:], lhsT=ftT[:, j - 1, e, :], rhs=wT[:, j - 1, cols, e],
+                            start=(j == 1 and e == 0), stop=False,
+                        )
+            nc.tensor.matmul(
+                out=ft2_sum[:], lhsT=ones[:], rhs=bias_rows[:, bfc2_at + half * BANK : bfc2_at + (half + 1) * BANK],
+                start=False, stop=True,
+            )
+            nc.scalar.copy(out=ft2[:, cols], in_=ft2_sum[:])
+
+        first_wave, second_wave = waves
+        sort_step(0)
+        first_convolution(range(0, CHUNKS + 1))
+        sorted_h = add_bias(first_wave[0], first_wave[1])
+        flip_text_features()
+        plain_layer(0)
+        flip_hidden(sorted_h)
+        plain_layer(1)
+        first_convolution(range(CHUNKS + 1, 2 * CHUNKS + 1))
+        sorted_h = add_bias(second_wave[0], second_wave[1])
+        pixel_sum = [sum_banks.tile([P, BANK], F32, tag="sum", name="pixel_sum") for half in range(HALVES)]
+        second_convolution(first_wave[0], first_wave[1], pixel_sum)
+        flip_hidden(sorted_h)
+        second_convolution(second_wave[0], second_wave[1], pixel_sum)
+
+        for half in range(HALVES):
+            cols = slice(half * BANK, (half + 1) * BANK)
+            pooled = stream.tile([P, BANK], F32, tag="pooled")
+            nc.vector.scalar_tensor_tensor(
+                out=pooled[:], in0=pixel_sum[half][:], scalar=1.0 / PIX, in1=bb_all[:, cols], op0=MULT, op1=ADD
+            )
+            gate = stream.tile([P, BANK], F32, tag="gate")
+            nc.scalar.activation(out=gate[:], in_=pooled[:], func=FUNC.Sigmoid)
+            gated = stream.tile([P, BANK], F32, tag="gated")
+            nc.vector.scalar_tensor_tensor(
+                out=gated[:], in0=gate[:], scalar=1.0, in1=ft2[:, cols], op0=ADD, op1=MULT
+            )
+            nc.sync.dma_start(out=out[:, cols], in_=gated[:])

@@ -112,12 +112,11 @@ def tile_joint_module_pb_kernel(tc, fv, ft, Wa_words, Wa_scales, ba, Wb_words, W
             )
             nc.scalar.copy(out=bb_all[:, half * BANK : (half + 1) * BANK], in_=spread[:])
 
-        def flip_and_quantise(sorted_tile, n, relu, codes, scales):
+        def flip_and_quantise(words, n, relu, codes, scales):
             bank = flip_banks.tile([P, PAIR, 2, P], F32, tag="flip")
             for x in range(n):
                 for u in range(2):
-                    words = sorted_tile[:, x, u].rearrange("b p e -> b (p e)").bitcast(F32)
-                    nc.tensor.transpose(out=bank[:, x, u, :], in_=words, identity=ident[:])
+                    nc.tensor.transpose(out=bank[:, x, u, :], in_=words[:, x, u, :], identity=ident[:])
             grouped = stream.tile([P, PAIR, P, PACK], BF16, tag="grouped", bufs=6, align_bytes=64)
             if relu:
                 for x in range(n):
@@ -147,19 +146,23 @@ def tile_joint_module_pb_kernel(tc, fv, ft, Wa_words, Wa_scales, ba, Wb_words, W
 
         def sort_step(i):
             first, count, g = steps[i]
-            sorted_fv[i] = []
-            for x0, n in pixel_runs(first, count, PAIR):
-                tile_x = stream.tile([P, PAIR, 2, P, 2], BF16, tag="sorted", bufs=6, name="sorted")
-                nc.vector.tensor_copy(
-                    out=tile_x[:, 0:n].rearrange("b x u p e -> b p x u e"),
-                    in_=raw[g][:].rearrange("b (p u e x) -> b p x u e", u=2, e=2, x=PIX)[:, :, x0 : x0 + n],
-                )
-                sorted_fv[i].append((x0, n, tile_x))
+            sorted_fv[i] = stream.tile([P, P, count, PACK], BF16, tag="sorted", bufs=2, name="sorted")
+            nc.vector.tensor_copy(
+                out=sorted_fv[i][:],
+                in_=raw[g][:].rearrange("b (p t x) -> b p x t", t=PACK, x=PIX)[:, :, first : first + count, :],
+            )
 
         def flip_step(i):
-            g = steps[i][2]
-            for x0, n, tile_x in sorted_fv[i]:
-                flip_and_quantise(tile_x, n, False, fv_codes[:, g, x0 : x0 + n, :], fv_scales[:, g, x0 : x0 + n, :])
+            first, count, g = steps[i]
+            words = (
+                sorted_fv[i][:].rearrange("b p x t -> b (p x t)").bitcast(F32)
+                .rearrange("b (p x u) -> b x u p", x=count, u=2)
+            )
+            for x0, n in pixel_runs(first, count, PAIR):
+                flip_and_quantise(
+                    words[:, x0 - first : x0 - first + n], n, False,
+                    fv_codes[:, g, x0 : x0 + n, :], fv_scales[:, g, x0 : x0 + n, :],
+                )
 
         def multiply_step(i):
             first, count, g = steps[i]
@@ -204,7 +207,8 @@ def tile_joint_module_pb_kernel(tc, fv, ft, Wa_words, Wa_scales, ba, Wb_words, W
 
         def flip_hidden(sorted_h):
             for x0, n, tile_x in sorted_h:
-                flip_and_quantise(tile_x, n, True, h_codes[:, x0 : x0 + n, :], h_scales[:, x0 : x0 + n, :])
+                words = tile_x[:].rearrange("b x u p e -> b x u (p e)").bitcast(F32)
+                flip_and_quantise(words, n, True, h_codes[:, x0 : x0 + n, :], h_scales[:, x0 : x0 + n, :])
 
         def second_convolution(first, count, pixel_sum):
             for pix in range(first, first + count):

@@ -29,6 +29,7 @@ FLIP_BANKS = 3
 SUM_BANKS = 8 - FLIP_BANKS
 K_FC = C_OUT // (2 * P)
 W_TILES = BANK // P
+COVER_ADD = 3
 
 FLOPS = 2 * P * PIX * (C_IN * HID + HID * C_OUT) + 2 * P * C_OUT * C_OUT
 
@@ -77,6 +78,14 @@ def tile_joint_module_pb_kernel(tc, fv, ft, Wa_words, Wa_scales, ba, Wb_words, W
         def load_chunk(g):
             nc.sync.dma_start(out=raw[g][:], in_=fv_rows[:, g * row : (g + 1) * row])
 
+        w_rows = Wfc2.rearrange("(a r) c -> r a c", r=P)
+
+        def load_plain_weights(half):
+            a_range = slice(half * W_TILES, (half + 1) * W_TILES)
+            nc.sync.dma_start(out=w_sb[:, a_range, :], in_=w_rows[:, a_range, :])
+
+        nc.sync.dma_start(out=ft_sb[:], in_=ft)
+        load_plain_weights(0)
         load_chunk(0)
         load_chunk(1)
         for quad in range(4):
@@ -87,11 +96,7 @@ def tile_joint_module_pb_kernel(tc, fv, ft, Wa_words, Wa_scales, ba, Wb_words, W
         nc.sync.dma_start(out=wa_words[:].bitcast(I32), in_=Wa_words.bitcast(I32).rearrange("g p n -> p g n"))
         for g in range(2, CHUNKS):
             load_chunk(g)
-        nc.sync.dma_start(out=ft_sb[:], in_=ft)
-        w_rows = Wfc2.rearrange("(a r) c -> r a c", r=P)
-        for half in range(HALVES):
-            a_range = slice(half * W_TILES, (half + 1) * W_TILES)
-            nc.sync.dma_start(out=w_sb[:, a_range, :], in_=w_rows[:, a_range, :])
+        load_plain_weights(1)
         for quad in range(4):
             nc.sync.dma_start(
                 out=wb_planes[32 * quad : 32 * quad + 4].bitcast(I32),
@@ -112,25 +117,26 @@ def tile_joint_module_pb_kernel(tc, fv, ft, Wa_words, Wa_scales, ba, Wb_words, W
             )
             nc.scalar.copy(out=bb_all[:, half * BANK : (half + 1) * BANK], in_=spread[:])
 
-        def flip_and_quantise(words, n, relu, codes, scales):
+        def flip_and_quantise(words, n, relu_on, codes, scales):
             bank = flip_banks.tile([P, PAIR, 2, P], F32, tag="flip")
             for x in range(n):
                 for u in range(2):
                     nc.tensor.transpose(out=bank[:, x, u, :], in_=words[:, x, u, :], identity=ident[:])
             grouped = stream.tile([P, PAIR, P, PACK], BF16, tag="grouped", bufs=6, align_bytes=64)
-            if relu:
-                for x in range(n):
-                    nc.vector.tensor_scalar_max(
-                        out=grouped[:, x].rearrange("p b (u e) -> p b u e", u=2),
-                        in0=bank[:, x].bitcast(BF16).rearrange("p u (b e) -> p b u e", e=2),
-                        scalar1=0.0,
-                    )
-            else:
+            if relu_on is None:
                 nc.scalar.copy(
                     out=grouped[:, 0:n].rearrange("p x b t -> p (x b t)").bitcast(F32)
                     .rearrange("p (x b u) -> p x b u", x=n, u=2),
                     in_=bank[:, 0:n].rearrange("p x u b -> p x b u"),
                 )
+            else:
+                for x in range(n):
+                    h_out = grouped[:, x].rearrange("p b (u e) -> p b u e", u=2)
+                    h_in = bank[:, x].bitcast(BF16).rearrange("p u (b e) -> p b u e", e=2)
+                    if relu_on == "vector":
+                        nc.vector.tensor_scalar_max(out=h_out, in0=h_in, scalar1=0.0)
+                    else:
+                        nc.scalar.activation(out=h_out, in_=h_in, func=FUNC.Relu)
             nc.vector.quantize_mx(
                 out=codes.rearrange("p x b -> p (x b)").bitcast(FP8X4),
                 scales=scales.rearrange("p x b -> p (x b)"),
@@ -160,7 +166,7 @@ def tile_joint_module_pb_kernel(tc, fv, ft, Wa_words, Wa_scales, ba, Wb_words, W
             )
             for x0, n in pixel_runs(first, count, PAIR):
                 flip_and_quantise(
-                    words[:, x0 - first : x0 - first + n], n, False,
+                    words[:, x0 - first : x0 - first + n], n, None,
                     fv_codes[:, g, x0 : x0 + n, :], fv_scales[:, g, x0 : x0 + n, :],
                 )
 
@@ -206,13 +212,14 @@ def tile_joint_module_pb_kernel(tc, fv, ft, Wa_words, Wa_scales, ba, Wb_words, W
             return sorted_h
 
         def flip_hidden(sorted_h):
-            for x0, n, tile_x in sorted_h:
+            for k, (x0, n, tile_x) in enumerate(sorted_h):
+                relu_on = "vector" if k % 2 == 0 else "scalar"
                 words = tile_x[:].rearrange("b x u p e -> b x u (p e)").bitcast(F32)
-                flip_and_quantise(words, n, True, h_codes[:, x0 : x0 + n, :], h_scales[:, x0 : x0 + n, :])
+                flip_and_quantise(words, n, relu_on, h_codes[:, x0 : x0 + n, :], h_scales[:, x0 : x0 + n, :])
 
         def second_convolution(first, count, pixel_sum):
-            for pix in range(first, first + count):
-                for half in range(HALVES):
+            for half in range(HALVES):
+                for pix in range(first, first + count):
                     nc.tensor.matmul_mx(
                         out=pixel_sum[half][:],
                         lhsT=h_codes[:, pix, :].bitcast(FP8X4),
@@ -262,18 +269,19 @@ def tile_joint_module_pb_kernel(tc, fv, ft, Wa_words, Wa_scales, ba, Wb_words, W
             nc.scalar.copy(out=ft2[:, cols], in_=ft2_sum[:])
 
         first_wave, second_wave = waves
+        flip_text_features()
+        plain_layer(0)
         sort_step(0)
         first_convolution(range(0, CHUNKS + 1))
         sorted_h = add_bias(first_wave[0], first_wave[1])
-        flip_text_features()
-        plain_layer(0)
-        flip_hidden(sorted_h)
         plain_layer(1)
+        flip_hidden(sorted_h)
         first_convolution(range(CHUNKS + 1, 2 * CHUNKS + 1))
         sorted_h = add_bias(second_wave[0], second_wave[1])
         pixel_sum = [sum_banks.tile([P, BANK], F32, tag="sum", name="pixel_sum") for half in range(HALVES)]
-        second_convolution(first_wave[0], first_wave[1], pixel_sum)
+        second_convolution(first_wave[0], COVER_ADD, pixel_sum)
         flip_hidden(sorted_h)
+        second_convolution(first_wave[0] + COVER_ADD, first_wave[1] - COVER_ADD, pixel_sum)
         second_convolution(second_wave[0], second_wave[1], pixel_sum)
 
         for half in range(HALVES):

@@ -185,12 +185,14 @@ def tile_joint_module_pb_kernel(tc, fv, ft, Wa_words, Wa_scales, ba, Wb_words, W
                     stop=(g == CHUNKS - 1),
                 )
 
-        def first_convolution(rounds):
+        def first_convolution(rounds, between=None):
             for i in rounds:
                 if i + 1 < len(steps):
                     sort_step(i + 1)
                 if i < len(steps):
                     flip_step(i)
+                if between is not None:
+                    between(i)
                 if i >= 1:
                     multiply_step(i - 1)
 
@@ -216,6 +218,15 @@ def tile_joint_module_pb_kernel(tc, fv, ft, Wa_words, Wa_scales, ba, Wb_words, W
                 relu_on = "vector" if k % 2 == 0 else "scalar"
                 words = tile_x[:].rearrange("b x u p e -> b x u (p e)").bitcast(F32)
                 flip_and_quantise(words, n, relu_on, h_codes[:, x0 : x0 + n, :], h_scales[:, x0 : x0 + n, :])
+
+        def flip_hidden_pixel(sorted_h, pix, relu_on):
+            for x0, n, tile_x in sorted_h:
+                if x0 <= pix < x0 + n:
+                    words = tile_x[:].rearrange("b x u p e -> b x u (p e)").bitcast(F32)
+                    flip_and_quantise(
+                        words[:, pix - x0 : pix - x0 + 1], 1, relu_on,
+                        h_codes[:, pix : pix + 1, :], h_scales[:, pix : pix + 1, :],
+                    )
 
         def second_convolution(first, count, pixel_sum):
             for half in range(HALVES):
@@ -275,25 +286,36 @@ def tile_joint_module_pb_kernel(tc, fv, ft, Wa_words, Wa_scales, ba, Wb_words, W
         first_convolution(range(0, CHUNKS + 1))
         sorted_h = add_bias(first_wave[0], first_wave[1])
         plain_layer(1)
-        flip_hidden(sorted_h)
-        first_convolution(range(CHUNKS + 1, 2 * CHUNKS + 1))
+        first_hidden = sorted_h
+
+        def one_hidden_pixel(i):
+            pix = first_wave[0] + i - (CHUNKS + 1)
+            if pix < first_wave[0] + first_wave[1]:
+                flip_hidden_pixel(first_hidden, pix, "scalar")
+
+        first_convolution(range(CHUNKS + 1, 2 * CHUNKS + 1), one_hidden_pixel)
         sorted_h = add_bias(second_wave[0], second_wave[1])
         pixel_sum = [sum_banks.tile([P, BANK], F32, tag="sum", name="pixel_sum") for half in range(HALVES)]
         second_convolution(first_wave[0], COVER_ADD, pixel_sum)
         flip_hidden(sorted_h)
         second_convolution(first_wave[0] + COVER_ADD, first_wave[1] - COVER_ADD, pixel_sum)
-        second_convolution(second_wave[0], second_wave[1], pixel_sum)
+        for x0, n in pixel_runs(second_wave[0], second_wave[1], PAIR):
+            second_convolution(x0, n, pixel_sum)
 
-        for half in range(HALVES):
-            cols = slice(half * BANK, (half + 1) * BANK)
-            pooled = stream.tile([P, BANK], F32, tag="pooled")
+        halves = [slice(half * BANK, (half + 1) * BANK) for half in range(HALVES)]
+        pooled = []
+        for half, cols in enumerate(halves):
+            pooled.append(stream.tile([P, BANK], F32, tag="pooled", name="pooled"))
             nc.vector.scalar_tensor_tensor(
-                out=pooled[:], in0=pixel_sum[half][:], scalar=1.0 / PIX, in1=bb_all[:, cols], op0=MULT, op1=ADD
+                out=pooled[half][:], in0=pixel_sum[half][:], scalar=1.0 / PIX, in1=bb_all[:, cols], op0=MULT, op1=ADD
             )
-            gate = stream.tile([P, BANK], F32, tag="gate")
-            nc.scalar.activation(out=gate[:], in_=pooled[:], func=FUNC.Sigmoid)
+        gate = []
+        for half in range(HALVES):
+            gate.append(stream.tile([P, BANK], F32, tag="gate", name="gate"))
+            nc.scalar.activation(out=gate[half][:], in_=pooled[half][:], func=FUNC.Sigmoid)
+        for half, cols in enumerate(halves):
             gated = stream.tile([P, BANK], F32, tag="gated")
             nc.vector.scalar_tensor_tensor(
-                out=gated[:], in0=gate[:], scalar=1.0, in1=ft2[:, cols], op0=ADD, op1=MULT
+                out=gated[:], in0=gate[half][:], scalar=1.0, in1=ft2[:, cols], op0=ADD, op1=MULT
             )
             nc.sync.dma_start(out=out[:, cols], in_=gated[:])

@@ -29,6 +29,7 @@ FLIP_BANKS = 3
 SUM_BANKS = 8 - FLIP_BANKS
 K_FC = C_OUT // (2 * P)
 W_TILES = BANK // P
+PIECE = 256
 COVER_ADD = 3
 
 FLOPS = 2 * P * PIX * (C_IN * HID + HID * C_OUT) + 2 * P * C_OUT * C_OUT
@@ -302,20 +303,23 @@ def tile_joint_module_pb_kernel(tc, fv, ft, Wa_words, Wa_scales, ba, Wb_words, W
         for x0, n in pixel_runs(second_wave[0], second_wave[1], PAIR):
             second_convolution(x0, n, pixel_sum)
 
-        halves = [slice(half * BANK, (half + 1) * BANK) for half in range(HALVES)]
-        pooled = []
-        for half, cols in enumerate(halves):
-            pooled.append(stream.tile([P, BANK], F32, tag="pooled", name="pooled"))
+        pieces = [(half, slice(c0, c0 + PIECE)) for half in range(HALVES) for c0 in range(0, BANK, PIECE)]
+        pooled = stream.tile([P, C_OUT], F32, tag="pooled", bufs=1)
+        gate = stream.tile([P, C_OUT], F32, tag="gate", bufs=1)
+        gated = stream.tile([P, C_OUT], F32, tag="gated", bufs=1)
+
+        def columns(half, part):
+            return slice(half * BANK + part.start, half * BANK + part.stop)
+
+        for half, part in pieces:
+            cols = columns(half, part)
             nc.vector.scalar_tensor_tensor(
-                out=pooled[half][:], in0=pixel_sum[half][:], scalar=1.0 / PIX, in1=bb_all[:, cols], op0=MULT, op1=ADD
+                out=pooled[:, cols], in0=pixel_sum[half][:, part], scalar=1.0 / PIX, in1=bb_all[:, cols], op0=MULT, op1=ADD
             )
-        gate = []
-        for half in range(HALVES):
-            gate.append(stream.tile([P, BANK], F32, tag="gate", name="gate"))
-            nc.scalar.activation(out=gate[half][:], in_=pooled[half][:], func=FUNC.Sigmoid)
-        for half, cols in enumerate(halves):
-            gated = stream.tile([P, BANK], F32, tag="gated")
+            nc.scalar.activation(out=gate[:, cols], in_=pooled[:, cols], func=FUNC.Sigmoid)
+        for half, part in pieces:
+            cols = columns(half, part)
             nc.vector.scalar_tensor_tensor(
-                out=gated[:], in0=gate[half][:], scalar=1.0, in1=ft2[:, cols], op0=ADD, op1=MULT
+                out=gated[:, cols], in0=gate[:, cols], scalar=1.0, in1=ft2[:, cols], op0=ADD, op1=MULT
             )
-            nc.sync.dma_start(out=out[:, cols], in_=gated[:])
+            nc.sync.dma_start(out=out[:, cols], in_=gated[:, cols])

@@ -155,8 +155,8 @@ def tile_joint_module_pb_kernel(tc, fv, ft, Wa_words, Wa_scales, ba, Wb_words, W
             first, count, g = steps[i]
             sorted_fv[i] = stream.tile([P, P, count, PACK], BF16, tag="sorted", bufs=2, name="sorted")
             nc.vector.tensor_copy(
-                out=sorted_fv[i][:],
-                in_=raw[g][:].rearrange("b (p t x) -> b p x t", t=PACK, x=PIX)[:, :, first : first + count, :],
+                out=sorted_fv[i][:].rearrange("b p x t -> b p t x"),
+                in_=raw[g][:].rearrange("b (p t x) -> b p t x", t=PACK, x=PIX)[:, :, :, first : first + count],
             )
 
         def flip_step(i):

@@ -86,8 +86,8 @@ def tile_joint_module_pb_kernel(tc, fv, ft, Wa_words, Wa_scales, ba, Wb_words, W
             nc.sync.dma_start(out=w_sb[:, a_range, :], in_=w_rows[:, a_range, :])
 
         nc.sync.dma_start(out=ft_sb[:], in_=ft)
-        load_plain_weights(0)
         load_chunk(0)
+        load_plain_weights(0)
         load_chunk(1)
         for quad in range(4):
             nc.sync.dma_start(
@@ -107,16 +107,18 @@ def tile_joint_module_pb_kernel(tc, fv, ft, Wa_words, Wa_scales, ba, Wb_words, W
 
         ba_all = keep.tile([P, HID], F32)
         bb_all = keep.tile([P, C_OUT], F32)
-        spread = sum_banks.tile([P, BANK], F32, tag="sum")
-        nc.tensor.matmul(out=spread[:], lhsT=ones[:], rhs=bias_rows[:, 0:HID], start=True, stop=True)
-        nc.scalar.copy(out=ba_all[:], in_=spread[:])
-        for half in range(HALVES):
+
+        def spread_biases():
             spread = sum_banks.tile([P, BANK], F32, tag="sum")
-            nc.tensor.matmul(
-                out=spread[:], lhsT=ones[:], rhs=bias_rows[:, bb_at + half * BANK : bb_at + (half + 1) * BANK],
-                start=True, stop=True,
-            )
-            nc.scalar.copy(out=bb_all[:, half * BANK : (half + 1) * BANK], in_=spread[:])
+            nc.tensor.matmul(out=spread[:], lhsT=ones[:], rhs=bias_rows[:, 0:HID], start=True, stop=True)
+            nc.scalar.copy(out=ba_all[:], in_=spread[:])
+            for half in range(HALVES):
+                spread = sum_banks.tile([P, BANK], F32, tag="sum")
+                nc.tensor.matmul(
+                    out=spread[:], lhsT=ones[:], rhs=bias_rows[:, bb_at + half * BANK : bb_at + (half + 1) * BANK],
+                    start=True, stop=True,
+                )
+                nc.scalar.copy(out=bb_all[:, half * BANK : (half + 1) * BANK], in_=spread[:])
 
         def flip_and_quantise(words, n, relu_on, codes, scales):
             bank = flip_banks.tile([P, PAIR, 2, P], F32, tag="flip")
@@ -188,7 +190,7 @@ def tile_joint_module_pb_kernel(tc, fv, ft, Wa_words, Wa_scales, ba, Wb_words, W
 
         def first_convolution(rounds, between=None):
             for i in rounds:
-                if i + 1 < len(steps):
+                if i + 1 < len(steps) and i + 1 not in sorted_fv:
                     sort_step(i + 1)
                 if i < len(steps):
                     flip_step(i)
@@ -282,9 +284,12 @@ def tile_joint_module_pb_kernel(tc, fv, ft, Wa_words, Wa_scales, ba, Wb_words, W
 
         first_wave, second_wave = waves
         flip_text_features()
-        plain_layer(0)
         sort_step(0)
-        first_convolution(range(0, CHUNKS + 1))
+        flip_step(0)
+        plain_layer(0)
+        spread_biases()
+        sort_step(1)
+        first_convolution(range(1, CHUNKS + 1))
         sorted_h = add_bias(first_wave[0], first_wave[1])
         plain_layer(1)
         first_hidden = sorted_h

@@ -155,17 +155,17 @@ def tile_joint_module_pb_kernel(tc, fv, ft, Wa_words, Wa_scales, ba, Wb_words, W
 
         def sort_step(i):
             first, count, g = steps[i]
-            sorted_fv[i] = stream.tile([P, P, count, PACK], BF16, tag="sorted", bufs=2, name="sorted")
+            sorted_fv[i] = stream.tile([P, P, 2, count, 2], BF16, tag="sorted", bufs=2, name="sorted")
             nc.vector.tensor_copy(
-                out=sorted_fv[i][:].rearrange("b p x t -> b p t x"),
-                in_=raw[g][:].rearrange("b (p t x) -> b p t x", t=PACK, x=PIX)[:, :, :, first : first + count],
+                out=sorted_fv[i][:].rearrange("b p u x e -> b p u e x"),
+                in_=raw[g][:].rearrange("b (p u e x) -> b p u e x", u=2, e=2, x=PIX)[:, :, :, :, first : first + count],
             )
 
         def flip_step(i):
             first, count, g = steps[i]
             words = (
-                sorted_fv[i][:].rearrange("b p x t -> b (p x t)").bitcast(F32)
-                .rearrange("b (p x u) -> b x u p", x=count, u=2)
+                sorted_fv[i][:].rearrange("b p u x e -> b (p u x e)").bitcast(F32)
+                .rearrange("b (p u x) -> b x u p", x=count, u=2)
             )
             for x0, n in pixel_runs(first, count, PAIR):
                 flip_and_quantise(

@@ -30,6 +30,7 @@ SUM_BANKS = 8 - FLIP_BANKS
 K_FC = C_OUT // (2 * P)
 W_TILES = BANK // P
 PIECE = 256
+SORT_RUNS = {5: ((0, 2), (2, 3)), 4: ((0, 4),)}
 COVER_ADD = 3
 
 FLOPS = 2 * P * PIX * (C_IN * HID + HID * C_OUT) + 2 * P * C_OUT * C_OUT
@@ -155,17 +156,20 @@ def tile_joint_module_pb_kernel(tc, fv, ft, Wa_words, Wa_scales, ba, Wb_words, W
 
         def sort_step(i):
             first, count, g = steps[i]
-            sorted_fv[i] = stream.tile([P, P, 2, count, 2], BF16, tag="sorted", bufs=2, name="sorted")
-            nc.vector.tensor_copy(
-                out=sorted_fv[i][:].rearrange("b p u x e -> b p u e x"),
-                in_=raw[g][:].rearrange("b (p u e x) -> b p u e x", u=2, e=2, x=PIX)[:, :, :, :, first : first + count],
-            )
+            sorted_fv[i] = stream.tile([P, count, 2, P, 2], BF16, tag="sorted", bufs=2, name="sorted")
+            for x0, n in SORT_RUNS[count]:
+                nc.vector.tensor_copy(
+                    out=sorted_fv[i][:, x0 : x0 + n].rearrange("b x u p e -> b u p e x"),
+                    in_=raw[g][:].rearrange("b (p u e x) -> b u p e x", u=2, e=2, x=PIX)[
+                        :, :, :, :, first + x0 : first + x0 + n
+                    ],
+                )
 
         def flip_step(i):
             first, count, g = steps[i]
             words = (
-                sorted_fv[i][:].rearrange("b p u x e -> b (p u x e)").bitcast(F32)
-                .rearrange("b (p u x) -> b x u p", x=count, u=2)
+                sorted_fv[i][:].rearrange("b x u p e -> b (x u p e)").bitcast(F32)
+                .rearrange("b (x u p) -> b x u p", x=count, u=2)
             )
             for x0, n in pixel_runs(first, count, PAIR):
                 flip_and_quantise(

@@ -24,6 +24,8 @@ PIX = 9
 CHUNKS = C_IN // K_PASS
 BANK = 512
 HALVES = C_OUT // BANK
+GROUPED_BUFS = 7
+AHEAD2 = 2
 PAIR = 2
 FLIP_BANKS = 3
 SUM_BANKS = 8 - FLIP_BANKS
@@ -49,13 +51,9 @@ def tile_joint_module_pb_kernel(tc, fv, ft, Wa_words, Wa_scales, ba, Wb_words, W
         flip_banks = ctx.enter_context(tc.psum_pool(name="flip_banks", bufs=FLIP_BANKS))
         sum_banks = ctx.enter_context(tc.psum_pool(name="sum_banks", bufs=SUM_BANKS))
 
-        bias_rows = keep.tile([P, HID + 2 * C_OUT], BF16)
-        nc.vector.memset(bias_rows[:].bitcast(I32), 0)
-        bb_at = HID
-        bfc2_at = HID + C_OUT
-        nc.scalar.dma_start(out=bias_rows[0:1, 0:HID], in_=ba.rearrange("(o n) -> o n", o=1))
-        nc.scalar.dma_start(out=bias_rows[0:1, bb_at : bb_at + C_OUT], in_=bb.rearrange("(o n) -> o n", o=1))
-        nc.scalar.dma_start(out=bias_rows[0:1, bfc2_at : bfc2_at + C_OUT], in_=bfc2.rearrange("(o n) -> o n", o=1))
+        ba_row = keep.tile([P, HID], BF16)
+        nc.vector.memset(ba_row[:].bitcast(I32), 0)
+        nc.scalar.dma_start(out=ba_row[0:1, :], in_=ba.rearrange("(o n) -> o n", o=1))
         ident = keep.tile([P, P], F32)
         make_identity(nc, ident[:])
         ones = keep.tile([P, P], BF16)
@@ -82,51 +80,64 @@ def tile_joint_module_pb_kernel(tc, fv, ft, Wa_words, Wa_scales, ba, Wb_words, W
 
         w_rows = Wfc2.rearrange("(a r) c -> r a c", r=P)
 
-        def load_plain_weights(half):
+        def load_plain_weights(half, part=0, parts=1):
             a_range = slice(half * W_TILES, (half + 1) * W_TILES)
-            nc.sync.dma_start(out=w_sb[:, a_range, :], in_=w_rows[:, a_range, :])
+            cols = slice(part * C_OUT // parts, (part + 1) * C_OUT // parts)
+            nc.sync.dma_start(out=w_sb[:, a_range, cols], in_=w_rows[:, a_range, cols])
 
-        nc.sync.dma_start(out=ft_sb[:], in_=ft)
+        def load_ft():
+            nc.sync.dma_start(out=ft_sb[:], in_=ft)
+
+        def load_wa_scales():
+            for quad in range(4):
+                nc.sync.dma_start(
+                    out=wa_planes[32 * quad : 32 * quad + 4].bitcast(I32),
+                    in_=Wa_scales.bitcast(I32)[:, 4 * quad : 4 * quad + 4, :].rearrange("g r n -> r g n"),
+                )
+
+        def load_wa_words(g0=0, g1=CHUNKS):
+            nc.sync.dma_start(
+                out=wa_words[:, g0:g1, :].bitcast(I32), in_=Wa_words.bitcast(I32)[g0:g1].rearrange("g p n -> p g n")
+            )
+
+        def load_wb():
+            for quad in range(4):
+                nc.sync.dma_start(
+                    out=wb_planes[32 * quad : 32 * quad + 4].bitcast(I32),
+                    in_=Wb_scales.bitcast(I32)[0, 4 * quad : 4 * quad + 4, :],
+                )
+            nc.sync.dma_start(out=wb_words[:].bitcast(I32), in_=Wb_words.bitcast(I32)[0])
+
+        load_ft()
+        load_plain_weights(0, 0, 2)
+        load_plain_weights(0, 1, 2)
         load_chunk(0)
-        load_plain_weights(0)
-        load_chunk(1)
-        for quad in range(4):
-            nc.sync.dma_start(
-                out=wa_planes[32 * quad : 32 * quad + 4].bitcast(I32),
-                in_=Wa_scales.bitcast(I32)[:, 4 * quad : 4 * quad + 4, :].rearrange("g r n -> r g n"),
-            )
-        nc.sync.dma_start(out=wa_words[:].bitcast(I32), in_=Wa_words.bitcast(I32).rearrange("g p n -> p g n"))
-        for g in range(2, CHUNKS):
+        load_wa_scales()
+        for g in range(1, CHUNKS, 2):
             load_chunk(g)
+            load_wa_words(g - 1, g + 1)
+            if g + 1 < CHUNKS:
+                load_chunk(g + 1)
         load_plain_weights(1)
-        for quad in range(4):
-            nc.sync.dma_start(
-                out=wb_planes[32 * quad : 32 * quad + 4].bitcast(I32),
-                in_=Wb_scales.bitcast(I32)[0, 4 * quad : 4 * quad + 4, :],
-            )
-        nc.sync.dma_start(out=wb_words[:].bitcast(I32), in_=Wb_words.bitcast(I32)[0])
+        load_wb()
+        bb_all = keep.tile([P, C_OUT], BF16)
+        bfc2_all = keep.tile([P, C_OUT], BF16)
+        nc.sync.dma_start(out=bb_all[:], in_=bb.partition_broadcast(P))
+        nc.sync.dma_start(out=bfc2_all[:], in_=bfc2.partition_broadcast(P))
 
         ba_all = keep.tile([P, HID], F32)
-        bb_all = keep.tile([P, C_OUT], F32)
 
-        def spread_biases():
+        def spread_ba():
             spread = sum_banks.tile([P, BANK], F32, tag="sum")
-            nc.tensor.matmul(out=spread[:], lhsT=ones[:], rhs=bias_rows[:, 0:HID], start=True, stop=True)
+            nc.tensor.matmul(out=spread[:], lhsT=ones[:], rhs=ba_row[:], start=True, stop=True)
             nc.scalar.copy(out=ba_all[:], in_=spread[:])
-            for half in range(HALVES):
-                spread = sum_banks.tile([P, BANK], F32, tag="sum")
-                nc.tensor.matmul(
-                    out=spread[:], lhsT=ones[:], rhs=bias_rows[:, bb_at + half * BANK : bb_at + (half + 1) * BANK],
-                    start=True, stop=True,
-                )
-                nc.scalar.copy(out=bb_all[:, half * BANK : (half + 1) * BANK], in_=spread[:])
 
-        def flip_and_quantise(words, n, relu_on, codes, scales):
+        def flip(words, n, relu_on):
             bank = flip_banks.tile([P, PAIR, 2, P], F32, tag="flip")
             for x in range(n):
                 for u in range(2):
                     nc.tensor.transpose(out=bank[:, x, u, :], in_=words[:, x, u, :], identity=ident[:])
-            grouped = stream.tile([P, PAIR, P, PACK], BF16, tag="grouped", bufs=6, align_bytes=64)
+            grouped = stream.tile([P, PAIR, P, PACK], BF16, tag="grouped", bufs=GROUPED_BUFS, align_bytes=64)
             if relu_on is None:
                 nc.scalar.copy(
                     out=grouped[:, 0:n].rearrange("p x b t -> p (x b t)").bitcast(F32)
@@ -141,22 +152,29 @@ def tile_joint_module_pb_kernel(tc, fv, ft, Wa_words, Wa_scales, ba, Wb_words, W
                         nc.vector.tensor_scalar_max(out=h_out, in0=h_in, scalar1=0.0)
                     else:
                         nc.scalar.activation(out=h_out, in_=h_in, func=FUNC.Relu)
+            return grouped
+
+        def quantise(grouped, n, codes, scales):
             nc.vector.quantize_mx(
                 out=codes.rearrange("p x b -> p (x b)").bitcast(FP8X4),
                 scales=scales.rearrange("p x b -> p (x b)"),
                 in_=grouped[:, 0:n].rearrange("p x b t -> p (x b t)"),
             )
 
+        def flip_and_quantise(words, n, relu_on, codes, scales):
+            quantise(flip(words, n, relu_on), n, codes, scales)
+
         fv_codes = keep.tile([P, CHUNKS, PIX, P], U32, align_bytes=64)
         fv_scales = keep.tile([P, CHUNKS, PIX, P], U8, align_bytes=64)
         waves = pixel_runs(0, PIX, SUM_BANKS)
         steps = [(first, count, g) for first, count in waves for g in range(CHUNKS)]
         sorted_fv = {}
+        grouped_fv = {}
         hidden = {}
 
         def sort_step(i):
             first, count, g = steps[i]
-            sorted_fv[i] = stream.tile([P, count, 2, P, 2], BF16, tag="sorted", bufs=2, name="sorted")
+            sorted_fv[i] = stream.tile([P, count, 2, P, 2], BF16, tag="sorted", bufs=3, name="sorted")
             for x0, n in SORT_RUNS[count]:
                 nc.vector.tensor_copy(
                     out=sorted_fv[i][:, x0 : x0 + n].rearrange("b x u p e -> b u p e x"),
@@ -171,11 +189,14 @@ def tile_joint_module_pb_kernel(tc, fv, ft, Wa_words, Wa_scales, ba, Wb_words, W
                 sorted_fv[i][:].rearrange("b x u p e -> b (x u p e)").bitcast(F32)
                 .rearrange("b (x u p) -> b x u p", x=count, u=2)
             )
-            for x0, n in pixel_runs(first, count, PAIR):
-                flip_and_quantise(
-                    words[:, x0 - first : x0 - first + n], n, None,
-                    fv_codes[:, g, x0 : x0 + n, :], fv_scales[:, g, x0 : x0 + n, :],
-                )
+            grouped_fv[i] = [
+                (x0, n, flip(words[:, x0 - first : x0 - first + n], n, None)) for x0, n in pixel_runs(first, count, PAIR)
+            ]
+
+        def quantise_step(i):
+            first, count, g = steps[i]
+            for x0, n, grouped in grouped_fv[i]:
+                quantise(grouped, n, fv_codes[:, g, x0 : x0 + n, :], fv_scales[:, g, x0 : x0 + n, :])
 
         def multiply_step(i):
             first, count, g = steps[i]
@@ -192,14 +213,22 @@ def tile_joint_module_pb_kernel(tc, fv, ft, Wa_words, Wa_scales, ba, Wb_words, W
                     stop=(g == CHUNKS - 1),
                 )
 
-        def first_convolution(rounds, between=None):
+        def first_convolution(rounds, ahead, between=None, late=None):
             for i in rounds:
-                if i + 1 < len(steps) and i + 1 not in sorted_fv:
-                    sort_step(i + 1)
+                for k in range(i + 1, min(i + 2, len(steps))):
+                    if k not in sorted_fv:
+                        sort_step(k)
                 if i < len(steps):
                     flip_step(i)
                 if between is not None:
                     between(i)
+                if ahead == 2:
+                    if i + 2 < len(steps):
+                        sort_step(i + 2)
+                if late is not None:
+                    late(i)
+                if i < len(steps):
+                    quantise_step(i)
                 if i >= 1:
                     multiply_step(i - 1)
 
@@ -226,14 +255,17 @@ def tile_joint_module_pb_kernel(tc, fv, ft, Wa_words, Wa_scales, ba, Wb_words, W
                 words = tile_x[:].rearrange("b x u p e -> b x u (p e)").bitcast(F32)
                 flip_and_quantise(words, n, relu_on, h_codes[:, x0 : x0 + n, :], h_scales[:, x0 : x0 + n, :])
 
+        waiting_h = {}
+
+        def quantise_hidden_pixel(pix):
+            if pix in waiting_h:
+                quantise(waiting_h[pix], 1, h_codes[:, pix : pix + 1, :], h_scales[:, pix : pix + 1, :])
+
         def flip_hidden_pixel(sorted_h, pix, relu_on):
             for x0, n, tile_x in sorted_h:
                 if x0 <= pix < x0 + n:
                     words = tile_x[:].rearrange("b x u p e -> b x u (p e)").bitcast(F32)
-                    flip_and_quantise(
-                        words[:, pix - x0 : pix - x0 + 1], 1, relu_on,
-                        h_codes[:, pix : pix + 1, :], h_scales[:, pix : pix + 1, :],
-                    )
+                    waiting_h[pix] = flip(words[:, pix - x0 : pix - x0 + 1], 1, relu_on)
 
         def second_convolution(first, count, pixel_sum):
             for half in range(HALVES):
@@ -278,22 +310,19 @@ def tile_joint_module_pb_kernel(tc, fv, ft, Wa_words, Wa_scales, ba, Wb_words, W
                     for e in range(2):
                         nc.tensor.matmul(
                             out=ft2_sum[:], lhsT=ftT[:, j - 1, e, :], rhs=wT[:, j - 1, cols, e],
-                            start=(j == 1 and e == 0), stop=False,
+                            start=(j == 1 and e == 0), stop=(j == K_FC and e == 1),
                         )
-            nc.tensor.matmul(
-                out=ft2_sum[:], lhsT=ones[:], rhs=bias_rows[:, bfc2_at + half * BANK : bfc2_at + (half + 1) * BANK],
-                start=False, stop=True,
-            )
             nc.scalar.copy(out=ft2[:, cols], in_=ft2_sum[:])
 
         first_wave, second_wave = waves
         flip_text_features()
+        plain_layer(0)
+        spread_ba()
         sort_step(0)
         flip_step(0)
-        plain_layer(0)
-        spread_biases()
         sort_step(1)
-        first_convolution(range(1, CHUNKS + 1))
+        quantise_step(0)
+        first_convolution(range(1, CHUNKS + 1), 1)
         sorted_h = add_bias(first_wave[0], first_wave[1])
         plain_layer(1)
         first_hidden = sorted_h
@@ -303,7 +332,10 @@ def tile_joint_module_pb_kernel(tc, fv, ft, Wa_words, Wa_scales, ba, Wb_words, W
             if pix < first_wave[0] + first_wave[1]:
                 flip_hidden_pixel(first_hidden, pix, "scalar")
 
-        first_convolution(range(CHUNKS + 1, 2 * CHUNKS + 1), one_hidden_pixel)
+        def last_hidden_pixel(i):
+            quantise_hidden_pixel(first_wave[0] + i - 1 - (CHUNKS + 1))
+
+        first_convolution(range(CHUNKS + 1, 2 * CHUNKS + 1), AHEAD2, one_hidden_pixel, last_hidden_pixel)
         sorted_h = add_bias(second_wave[0], second_wave[1])
         pixel_sum = [sum_banks.tile([P, BANK], F32, tag="sum", name="pixel_sum") for half in range(HALVES)]
         second_convolution(first_wave[0], COVER_ADD, pixel_sum)
@@ -311,6 +343,7 @@ def tile_joint_module_pb_kernel(tc, fv, ft, Wa_words, Wa_scales, ba, Wb_words, W
         second_convolution(first_wave[0] + COVER_ADD, first_wave[1] - COVER_ADD, pixel_sum)
         for x0, n in pixel_runs(second_wave[0], second_wave[1], PAIR):
             second_convolution(x0, n, pixel_sum)
+        nc.vector.tensor_tensor(out=ft2[:], in0=ft2[:], in1=bfc2_all[:], op=ADD)
 
         pieces = [(half, slice(c0, c0 + PIECE)) for half in range(HALVES) for c0 in range(0, BANK, PIECE)]
         pooled = stream.tile([P, C_OUT], F32, tag="pooled", bufs=1)

@@ -24,15 +24,16 @@ PIX = 9
 CHUNKS = C_IN // K_PASS
 BANK = 512
 HALVES = C_OUT // BANK
-GROUPED_BUFS = 7
-AHEAD2 = 2
+GROUPED_BUFS = 8
 PAIR = 2
 FLIP_BANKS = 3
 SUM_BANKS = 8 - FLIP_BANKS
 K_FC = C_OUT // (2 * P)
 W_TILES = BANK // P
 PIECE = 256
-SORT_RUNS = {5: ((0, 2), (2, 3)), 4: ((0, 4),)}
+EARLY = 6
+LAST = 8
+EARLY_RUNS = ((0, 3), (3, 3))
 COVER_ADD = 3
 
 FLOPS = 2 * P * PIX * (C_IN * HID + HID * C_OUT) + 2 * P * C_OUT * C_OUT
@@ -132,8 +133,11 @@ def tile_joint_module_pb_kernel(tc, fv, ft, Wa_words, Wa_scales, ba, Wb_words, W
             nc.tensor.matmul(out=spread[:], lhsT=ones[:], rhs=ba_row[:], start=True, stop=True)
             nc.scalar.copy(out=ba_all[:], in_=spread[:])
 
-        def flip(words, n, relu_on):
-            bank = flip_banks.tile([P, PAIR, 2, P], F32, tag="flip")
+        def flip(words, n, relu_on, spare=False):
+            if spare:
+                bank = sum_banks.tile([P, PAIR, 2, P], F32, tag="sum")
+            else:
+                bank = flip_banks.tile([P, PAIR, 2, P], F32, tag="flip")
             for x in range(n):
                 for u in range(2):
                     nc.tensor.transpose(out=bank[:, x, u, :], in_=words[:, x, u, :], identity=ident[:])
@@ -161,111 +165,95 @@ def tile_joint_module_pb_kernel(tc, fv, ft, Wa_words, Wa_scales, ba, Wb_words, W
                 in_=grouped[:, 0:n].rearrange("p x b t -> p (x b t)"),
             )
 
-        def flip_and_quantise(words, n, relu_on, codes, scales):
-            quantise(flip(words, n, relu_on), n, codes, scales)
-
-        fv_codes = keep.tile([P, CHUNKS, PIX, P], U32, align_bytes=64)
-        fv_scales = keep.tile([P, CHUNKS, PIX, P], U8, align_bytes=64)
-        waves = pixel_runs(0, PIX, SUM_BANKS)
-        steps = [(first, count, g) for first, count in waves for g in range(CHUNKS)]
+        fv_codes = keep.tile([P, CHUNKS, LAST, P], U32, align_bytes=64)
+        fv_scales = keep.tile([P, CHUNKS, LAST, P], U8, align_bytes=64)
+        last_codes = keep.tile([P, CHUNKS, P], U32, align_bytes=64)
+        last_scales = keep.tile([P, CHUNKS, P], U8, align_bytes=64)
+        first_wave, second_wave = pixel_runs(0, PIX, SUM_BANKS)
         sorted_fv = {}
         grouped_fv = {}
         hidden = {}
 
-        def sort_step(i):
-            first, count, g = steps[i]
-            sorted_fv[i] = stream.tile([P, count, 2, P, 2], BF16, tag="sorted", bufs=3, name="sorted")
-            for x0, n in SORT_RUNS[count]:
-                nc.vector.tensor_copy(
-                    out=sorted_fv[i][:, x0 : x0 + n].rearrange("b x u p e -> b u p e x"),
-                    in_=raw[g][:].rearrange("b (p u e x) -> b u p e x", u=2, e=2, x=PIX)[
-                        :, :, :, :, first + x0 : first + x0 + n
-                    ],
-                )
-
-        def flip_step(i):
-            first, count, g = steps[i]
-            words = (
-                sorted_fv[i][:].rearrange("b x u p e -> b (x u p e)").bitcast(F32)
-                .rearrange("b (x u p) -> b x u p", x=count, u=2)
+        def sort_pixels(out, g, x0, n, rows=slice(0, P)):
+            nc.vector.tensor_copy(
+                out=out[:, :, :, rows, :].rearrange("b x u p e -> b u p e x"),
+                in_=raw[g][:].rearrange("b (p u e x) -> b u p e x", u=2, e=2, x=PIX)[:, :, rows, :, x0 : x0 + n],
             )
-            grouped_fv[i] = [
-                (x0, n, flip(words[:, x0 - first : x0 - first + n], n, None)) for x0, n in pixel_runs(first, count, PAIR)
+
+        def as_words(tile_x):
+            return tile_x.rearrange("b x u p e -> b x u (p e)").bitcast(F32)
+
+        def sort_early(g):
+            sorted_fv[g] = stream.tile([P, EARLY, 2, P, 2], BF16, tag="sorted", bufs=3, name="sorted")
+            for x0, n in EARLY_RUNS:
+                sort_pixels(sorted_fv[g][:, x0 : x0 + n], g, x0, n)
+
+        def flip_early(g):
+            words = as_words(sorted_fv[g][:])
+            grouped_fv[g] = [flip(words[:, x0 : x0 + PAIR], PAIR, None) for x0 in range(0, EARLY, PAIR)]
+
+        def quantise_early(g):
+            for grouped, x0 in zip(grouped_fv[g], range(0, EARLY, PAIR)):
+                quantise(grouped, PAIR, fv_codes[:, g, x0 : x0 + PAIR, :], fv_scales[:, g, x0 : x0 + PAIR, :])
+
+        def sort_late(g):
+            k = g // 2
+            if g % 2 == 0:
+                sorted_fv["late", k] = stream.tile([P, 2, 3, 2, P, 2], BF16, tag="sorted_late", bufs=2, name="sorted_late")
+            sort_pixels(sorted_fv["late", k][:, g % 2], g, EARLY, 3)
+
+        def flip_late(k):
+            both = sorted_fv["late", k]
+            words = both[:].rearrange("b s x u p e -> b s x u (p e)").bitcast(F32)
+            grouped_fv["late", k] = [
+                flip(words[:, 0, 0:PAIR], PAIR, None), flip(words[:, :, PAIR], 2, None), flip(words[:, 1, 0:PAIR], PAIR, None)
             ]
 
-        def quantise_step(i):
-            first, count, g = steps[i]
-            for x0, n, grouped in grouped_fv[i]:
-                quantise(grouped, n, fv_codes[:, g, x0 : x0 + n, :], fv_scales[:, g, x0 : x0 + n, :])
+        def quantise_late(k):
+            g = 2 * k
+            one, last, two = grouped_fv["late", k]
+            quantise(one, PAIR, fv_codes[:, g, EARLY:LAST, :], fv_scales[:, g, EARLY:LAST, :])
+            quantise(last, 2, last_codes[:, g : g + 2, :], last_scales[:, g : g + 2, :])
+            quantise(two, PAIR, fv_codes[:, g + 1, EARLY:LAST, :], fv_scales[:, g + 1, EARLY:LAST, :])
 
-        def multiply_step(i):
-            first, count, g = steps[i]
+        def multiply(g, wave):
+            first, count = wave
             for pix in range(first, first + count):
                 if g == 0:
                     hidden[pix] = sum_banks.tile([P, HID], F32, tag="sum", name="hidden")
+                codes, scales = (last_codes[:, g, :], last_scales[:, g, :]) if pix == LAST else (
+                    fv_codes[:, g, pix, :], fv_scales[:, g, pix, :]
+                )
                 nc.tensor.matmul_mx(
                     out=hidden[pix][:],
-                    lhsT=fv_codes[:, g, pix, :].bitcast(FP8X4),
-                    lhsT_scale=fv_scales[:, g, pix, :],
+                    lhsT=codes.bitcast(FP8X4),
+                    lhsT_scale=scales,
                     rhs=wa_words[:, g, :].bitcast(FP4X4),
                     rhs_scale=wa_planes[:, g, :],
                     start=(g == 0),
                     stop=(g == CHUNKS - 1),
                 )
 
-        def first_convolution(rounds, ahead, between=None, late=None):
-            for i in rounds:
-                for k in range(i + 1, min(i + 2, len(steps))):
-                    if k not in sorted_fv:
-                        sort_step(k)
-                if i < len(steps):
-                    flip_step(i)
-                if between is not None:
-                    between(i)
-                if ahead == 2:
-                    if i + 2 < len(steps):
-                        sort_step(i + 2)
-                if late is not None:
-                    late(i)
-                if i < len(steps):
-                    quantise_step(i)
-                if i >= 1:
-                    multiply_step(i - 1)
-
         h_codes = keep.tile([P, PIX, P], U32, align_bytes=64)
         h_scales = keep.tile([P, PIX, P], U8, align_bytes=64)
+        sorted_h = {}
+        grouped_h = {}
 
-        def add_bias(first, count):
-            sorted_h = []
-            for x0, n in pixel_runs(first, count, PAIR):
-                tile_x = stream.tile([P, PAIR, 2, P, 2], BF16, tag="sorted_h", bufs=3, name="sorted_h")
-                for x in range(n):
-                    nc.vector.tensor_tensor(
-                        out=tile_x[:, x],
-                        in0=hidden[x0 + x][:].rearrange("b (p u e) -> b u p e", u=2, e=2),
-                        in1=ba_all[:].rearrange("b (p u e) -> b u p e", u=2, e=2),
-                        op=ADD,
-                    )
-                sorted_h.append((x0, n, tile_x))
-            return sorted_h
+        def add_bias(x0, n):
+            sorted_h[x0] = stream.tile([P, PAIR, 2, P, 2], BF16, tag="sorted_h", bufs=4, name="sorted_h")
+            for x in range(n):
+                nc.vector.tensor_tensor(
+                    out=sorted_h[x0][:, x],
+                    in0=hidden[x0 + x][:].rearrange("b (p u e) -> b u p e", u=2, e=2),
+                    in1=ba_all[:].rearrange("b (p u e) -> b u p e", u=2, e=2),
+                    op=ADD,
+                )
 
-        def flip_hidden(sorted_h):
-            for k, (x0, n, tile_x) in enumerate(sorted_h):
-                relu_on = "vector" if k % 2 == 0 else "scalar"
-                words = tile_x[:].rearrange("b x u p e -> b x u (p e)").bitcast(F32)
-                flip_and_quantise(words, n, relu_on, h_codes[:, x0 : x0 + n, :], h_scales[:, x0 : x0 + n, :])
+        def flip_hidden(x0, n, relu_on, spare=False):
+            grouped_h[x0] = flip(as_words(sorted_h[x0][:]), n, relu_on, spare)
 
-        waiting_h = {}
-
-        def quantise_hidden_pixel(pix):
-            if pix in waiting_h:
-                quantise(waiting_h[pix], 1, h_codes[:, pix : pix + 1, :], h_scales[:, pix : pix + 1, :])
-
-        def flip_hidden_pixel(sorted_h, pix, relu_on):
-            for x0, n, tile_x in sorted_h:
-                if x0 <= pix < x0 + n:
-                    words = tile_x[:].rearrange("b x u p e -> b x u (p e)").bitcast(F32)
-                    waiting_h[pix] = flip(words[:, pix - x0 : pix - x0 + 1], 1, relu_on)
+        def quantise_hidden(x0, n):
+            quantise(grouped_h[x0], n, h_codes[:, x0 : x0 + n, :], h_scales[:, x0 : x0 + n, :])
 
         def second_convolution(first, count, pixel_sum):
             for half in range(HALVES):
@@ -314,35 +302,60 @@ def tile_joint_module_pb_kernel(tc, fv, ft, Wa_words, Wa_scales, ba, Wb_words, W
                         )
             nc.scalar.copy(out=ft2[:, cols], in_=ft2_sum[:])
 
-        first_wave, second_wave = waves
         flip_text_features()
         plain_layer(0)
         spread_ba()
-        sort_step(0)
-        flip_step(0)
-        sort_step(1)
-        quantise_step(0)
-        first_convolution(range(1, CHUNKS + 1), 1)
-        sorted_h = add_bias(first_wave[0], first_wave[1])
+        sort_early(0)
+        flip_early(0)
+        sort_early(1)
+        quantise_early(0)
+        for g in range(1, CHUNKS):
+            if g + 1 < CHUNKS:
+                sort_early(g + 1)
+            else:
+                sort_late(0)
+                sort_late(1)
+            flip_early(g)
+            quantise_early(g)
+            multiply(g - 1, first_wave)
+        flip_late(0)
+        quantise_late(0)
+        multiply(CHUNKS - 1, first_wave)
+        add_bias(0, PAIR)
+        add_bias(2, PAIR)
+        add_bias(4, 1)
         plain_layer(1)
-        first_hidden = sorted_h
-
-        def one_hidden_pixel(i):
-            pix = first_wave[0] + i - (CHUNKS + 1)
-            if pix < first_wave[0] + first_wave[1]:
-                flip_hidden_pixel(first_hidden, pix, "scalar")
-
-        def last_hidden_pixel(i):
-            quantise_hidden_pixel(first_wave[0] + i - 1 - (CHUNKS + 1))
-
-        first_convolution(range(CHUNKS + 1, 2 * CHUNKS + 1), AHEAD2, one_hidden_pixel, last_hidden_pixel)
-        sorted_h = add_bias(second_wave[0], second_wave[1])
+        sort_late(2)
+        sort_late(3)
+        flip_late(1)
+        flip_hidden(0, PAIR, "scalar", True)
+        sort_late(4)
+        quantise_late(1)
+        sort_late(5)
+        multiply(0, second_wave)
+        multiply(1, second_wave)
+        flip_late(2)
+        flip_hidden(2, PAIR, "scalar", True)
+        flip_hidden(4, 1, "scalar")
+        quantise_hidden(0, PAIR)
+        quantise_late(2)
+        multiply(2, second_wave)
+        multiply(3, second_wave)
+        quantise_hidden(2, PAIR)
+        multiply(4, second_wave)
+        multiply(5, second_wave)
+        quantise_hidden(4, 1)
+        add_bias(5, PAIR)
+        add_bias(7, PAIR)
         pixel_sum = [sum_banks.tile([P, BANK], F32, tag="sum", name="pixel_sum") for half in range(HALVES)]
-        second_convolution(first_wave[0], COVER_ADD, pixel_sum)
-        flip_hidden(sorted_h)
-        second_convolution(first_wave[0] + COVER_ADD, first_wave[1] - COVER_ADD, pixel_sum)
-        for x0, n in pixel_runs(second_wave[0], second_wave[1], PAIR):
-            second_convolution(x0, n, pixel_sum)
+        second_convolution(0, COVER_ADD, pixel_sum)
+        flip_hidden(5, PAIR, "vector")
+        quantise_hidden(5, PAIR)
+        flip_hidden(7, PAIR, "scalar")
+        quantise_hidden(7, PAIR)
+        second_convolution(COVER_ADD, first_wave[1] - COVER_ADD, pixel_sum)
+        for x0 in (5, 7):
+            second_convolution(x0, PAIR, pixel_sum)
         nc.vector.tensor_tensor(out=ft2[:], in0=ft2[:], in1=bfc2_all[:], op=ADD)
 
         pieces = [(half, slice(c0, c0 + PIECE)) for half in range(HALVES) for c0 in range(0, BANK, PIECE)]

@@ -74,17 +74,15 @@ def tile_joint_module_pb_kernel(tc, fv, ft, Wa_words, Wa_scales, ba, Wb_words, W
         wa_words = keep.tile([P, CHUNKS, 2 * HID], U8, align_bytes=64)
         wb_words = keep.tile([P, 2 * C_OUT], U8, align_bytes=64)
         ft_sb = keep.tile([P, C_OUT], BF16)
-        w_sb = keep.tile([P, HALVES * W_TILES, C_OUT], BF16)
+        w_sb = keep.tile([P, HALVES, W_TILES, C_OUT], BF16)
 
         def load_chunk(g):
             nc.sync.dma_start(out=raw[g][:], in_=fv_rows[:, g * row : (g + 1) * row])
 
-        w_rows = Wfc2.rearrange("(a r) c -> r a c", r=P)
+        w_rows = Wfc2.rearrange("(h r a) c -> h r a c", r=P, a=W_TILES)
 
-        def load_plain_weights(half, part=0, parts=1):
-            a_range = slice(half * W_TILES, (half + 1) * W_TILES)
-            cols = slice(part * C_OUT // parts, (part + 1) * C_OUT // parts)
-            nc.sync.dma_start(out=w_sb[:, a_range, cols], in_=w_rows[:, a_range, cols])
+        def load_plain_weights(half):
+            nc.sync.dma_start(out=w_sb[:, half], in_=w_rows[half])
 
         def load_ft():
             nc.sync.dma_start(out=ft_sb[:], in_=ft)
@@ -110,8 +108,7 @@ def tile_joint_module_pb_kernel(tc, fv, ft, Wa_words, Wa_scales, ba, Wb_words, W
             nc.sync.dma_start(out=wb_words[:].bitcast(I32), in_=Wb_words.bitcast(I32)[0])
 
         load_ft()
-        load_plain_weights(0, 0, 2)
-        load_plain_weights(0, 1, 2)
+        load_plain_weights(0)
         load_chunk(0)
         load_wa_scales()
         for g in range(1, CHUNKS, 2):
@@ -287,12 +284,13 @@ def tile_joint_module_pb_kernel(tc, fv, ft, Wa_words, Wa_scales, ba, Wb_words, W
                     for a in range(W_TILES):
                         nc.tensor.transpose(
                             out=bank[:, a, :],
-                            in_=w_sb[:, half * W_TILES + a, :].bitcast(F32)[:, j * P : (j + 1) * P],
+                            in_=w_sb[:, half, a, :].bitcast(F32)[:, j * P : (j + 1) * P],
                             identity=ident[:],
                         )
                     nc.scalar.copy(
-                        out=wT[:, j, cols, :].rearrange("q o e -> q (o e)").bitcast(F32),
-                        in_=bank[:].rearrange("q a r -> q (a r)"),
+                        out=wT[:, j, cols, :].rearrange("q o e -> q (o e)").bitcast(F32)
+                        .rearrange("q (r a) -> q r a", a=W_TILES),
+                        in_=bank[:].rearrange("q a r -> q r a"),
                     )
                 if j >= 1:
                     for e in range(2):

@@ -32,6 +32,8 @@ K_FC = C_OUT // (2 * P)
 W_TILES = BANK // P
 PIECE = 256
 EARLY = 6
+LOAD_PARTS = 2
+PLAIN_LAG = 2
 LAST = 8
 EARLY_RUNS = ((0, 3), (3, 3))
 COVER_ADD = 3
@@ -77,7 +79,12 @@ def tile_joint_module_pb_kernel(tc, fv, ft, Wa_words, Wa_scales, ba, Wb_words, W
         w_sb = keep.tile([P, HALVES, W_TILES, C_OUT], BF16)
 
         def load_chunk(g):
-            nc.sync.dma_start(out=raw[g][:], in_=fv_rows[:, g * row : (g + 1) * row])
+            piece = row // LOAD_PARTS
+            for k in range(LOAD_PARTS):
+                nc.sync.dma_start(
+                    out=raw[g][:, k * piece : (k + 1) * piece],
+                    in_=fv_rows[:, g * row + k * piece : g * row + (k + 1) * piece],
+                )
 
         w_rows = Wfc2.rearrange("(h r a) c -> h r a c", r=P, a=W_TILES)
 
@@ -182,8 +189,10 @@ def tile_joint_module_pb_kernel(tc, fv, ft, Wa_words, Wa_scales, ba, Wb_words, W
 
         def sort_early(g):
             sorted_fv[g] = stream.tile([P, EARLY, 2, P, 2], BF16, tag="sorted", bufs=3, name="sorted")
-            for x0, n in EARLY_RUNS:
-                sort_pixels(sorted_fv[g][:, x0 : x0 + n], g, x0, n)
+            for k in range(LOAD_PARTS):
+                rows = slice(k * P // LOAD_PARTS, (k + 1) * P // LOAD_PARTS)
+                for x0, n in EARLY_RUNS:
+                    sort_pixels(sorted_fv[g][:, x0 : x0 + n], g, x0, n, rows)
 
         def flip_early(g):
             words = as_words(sorted_fv[g][:])
@@ -278,7 +287,7 @@ def tile_joint_module_pb_kernel(tc, fv, ft, Wa_words, Wa_scales, ba, Wb_words, W
         def plain_layer(half):
             cols = slice(half * BANK, (half + 1) * BANK)
             ft2_sum = sum_banks.tile([P, BANK], F32, tag="sum")
-            for j in range(K_FC + 1):
+            for j in range(K_FC + PLAIN_LAG):
                 if j < K_FC:
                     bank = flip_banks.tile([P, W_TILES, P], F32, tag="flip")
                     for a in range(W_TILES):
@@ -292,11 +301,12 @@ def tile_joint_module_pb_kernel(tc, fv, ft, Wa_words, Wa_scales, ba, Wb_words, W
                         .rearrange("q (r a) -> q r a", a=W_TILES),
                         in_=bank[:].rearrange("q a r -> q r a"),
                     )
-                if j >= 1:
+                if j >= PLAIN_LAG:
+                    i = j - PLAIN_LAG
                     for e in range(2):
                         nc.tensor.matmul(
-                            out=ft2_sum[:], lhsT=ftT[:, j - 1, e, :], rhs=wT[:, j - 1, cols, e],
-                            start=(j == 1 and e == 0), stop=(j == K_FC and e == 1),
+                            out=ft2_sum[:], lhsT=ftT[:, i, e, :], rhs=wT[:, i, cols, e],
+                            start=(i == 0 and e == 0), stop=(i == K_FC - 1 and e == 1),
                         )
             nc.scalar.copy(out=ft2[:, cols], in_=ft2_sum[:])
 
@@ -320,11 +330,11 @@ def tile_joint_module_pb_kernel(tc, fv, ft, Wa_words, Wa_scales, ba, Wb_words, W
         quantise_late(0)
         multiply(CHUNKS - 1, first_wave)
         add_bias(0, PAIR)
+        sort_late(2)
         add_bias(2, PAIR)
+        sort_late(3)
         add_bias(4, 1)
         plain_layer(1)
-        sort_late(2)
-        sort_late(3)
         flip_late(1)
         flip_hidden(0, PAIR, "scalar", True)
         sort_late(4)

@@ -30,13 +30,13 @@ FLIP_BANKS = 3
 SUM_BANKS = 8 - FLIP_BANKS
 K_FC = C_OUT // (2 * P)
 W_TILES = BANK // P
-PIECE = 256
+PIECE = 128
 EARLY = 6
 LOAD_PARTS = 2
 PLAIN_LAG = 2
 LAST = 8
 EARLY_RUNS = ((0, 3), (3, 3))
-COVER_ADD = 3
+COVER_ADD = 2
 
 FLOPS = 2 * P * PIX * (C_IN * HID + HID * C_OUT) + 2 * P * C_OUT * C_OUT
 
@@ -114,9 +114,9 @@ def tile_joint_module_pb_kernel(tc, fv, ft, Wa_words, Wa_scales, ba, Wb_words, W
                 )
             nc.sync.dma_start(out=wb_words[:].bitcast(I32), in_=Wb_words.bitcast(I32)[0])
 
+        load_chunk(0)
         load_ft()
         load_plain_weights(0)
-        load_chunk(0)
         load_wa_scales()
         for g in range(1, CHUNKS, 2):
             load_chunk(g)
@@ -261,18 +261,17 @@ def tile_joint_module_pb_kernel(tc, fv, ft, Wa_words, Wa_scales, ba, Wb_words, W
         def quantise_hidden(x0, n):
             quantise(grouped_h[x0], n, h_codes[:, x0 : x0 + n, :], h_scales[:, x0 : x0 + n, :])
 
-        def second_convolution(first, count, pixel_sum):
-            for half in range(HALVES):
-                for pix in range(first, first + count):
-                    nc.tensor.matmul_mx(
-                        out=pixel_sum[half][:],
-                        lhsT=h_codes[:, pix, :].bitcast(FP8X4),
-                        lhsT_scale=h_scales[:, pix, :],
-                        rhs=wb_words[:, half * 2 * BANK : (half + 1) * 2 * BANK].bitcast(FP4X4),
-                        rhs_scale=wb_planes[:, half * BANK : (half + 1) * BANK],
-                        start=(pix == 0),
-                        stop=(pix == PIX - 1),
-                    )
+        def second_convolution(half, first, count):
+            for pix in range(first, first + count):
+                nc.tensor.matmul_mx(
+                    out=pixel_sum[half][:],
+                    lhsT=h_codes[:, pix, :].bitcast(FP8X4),
+                    lhsT_scale=h_scales[:, pix, :],
+                    rhs=wb_words[:, half * 2 * BANK : (half + 1) * 2 * BANK].bitcast(FP4X4),
+                    rhs_scale=wb_planes[:, half * BANK : (half + 1) * BANK],
+                    start=(pix == 0),
+                    stop=(pix == PIX - 1),
+                )
 
         ftT = keep.tile([P, K_FC, 2, P], BF16)
         wT = keep.tile([P, K_FC, C_OUT, 2], BF16)
@@ -310,18 +309,18 @@ def tile_joint_module_pb_kernel(tc, fv, ft, Wa_words, Wa_scales, ba, Wb_words, W
                         )
             nc.scalar.copy(out=ft2[:, cols], in_=ft2_sum[:])
 
+        sort_early(0)
+        flip_early(0)
+        quantise_early(0)
+        sort_late(0)
         flip_text_features()
         plain_layer(0)
         spread_ba()
-        sort_early(0)
-        flip_early(0)
         sort_early(1)
-        quantise_early(0)
         for g in range(1, CHUNKS):
             if g + 1 < CHUNKS:
                 sort_early(g + 1)
             else:
-                sort_late(0)
                 sort_late(1)
             flip_early(g)
             quantise_early(g)
@@ -350,39 +349,41 @@ def tile_joint_module_pb_kernel(tc, fv, ft, Wa_words, Wa_scales, ba, Wb_words, W
         multiply(2, second_wave)
         multiply(3, second_wave)
         quantise_hidden(2, PAIR)
-        multiply(4, second_wave)
-        multiply(5, second_wave)
+        for x0 in (5, 7):
+            multiply(4, (x0, PAIR))
+            multiply(5, (x0, PAIR))
         quantise_hidden(4, 1)
+        nc.vector.tensor_tensor(out=ft2[:], in0=ft2[:], in1=bfc2_all[:], op=ADD)
         add_bias(5, PAIR)
         add_bias(7, PAIR)
         pixel_sum = [sum_banks.tile([P, BANK], F32, tag="sum", name="pixel_sum") for half in range(HALVES)]
-        second_convolution(0, COVER_ADD, pixel_sum)
+        for half in range(HALVES):
+            second_convolution(half, 0, COVER_ADD)
         flip_hidden(5, PAIR, "vector")
         quantise_hidden(5, PAIR)
         flip_hidden(7, PAIR, "scalar")
         quantise_hidden(7, PAIR)
-        second_convolution(COVER_ADD, first_wave[1] - COVER_ADD, pixel_sum)
-        for x0 in (5, 7):
-            second_convolution(x0, PAIR, pixel_sum)
-        nc.vector.tensor_tensor(out=ft2[:], in0=ft2[:], in1=bfc2_all[:], op=ADD)
+        second_convolution(1, COVER_ADD, first_wave[1] - COVER_ADD)
+        second_convolution(0, COVER_ADD, PIX - COVER_ADD)
+        second_convolution(1, first_wave[1], second_wave[1])
 
-        pieces = [(half, slice(c0, c0 + PIECE)) for half in range(HALVES) for c0 in range(0, BANK, PIECE)]
         pooled = stream.tile([P, C_OUT], F32, tag="pooled", bufs=1)
         gate = stream.tile([P, C_OUT], F32, tag="gate", bufs=1)
         gated = stream.tile([P, C_OUT], F32, tag="gated", bufs=1)
-
-        def columns(half, part):
-            return slice(half * BANK + part.start, half * BANK + part.stop)
-
-        for half, part in pieces:
-            cols = columns(half, part)
-            nc.vector.scalar_tensor_tensor(
-                out=pooled[:, cols], in0=pixel_sum[half][:, part], scalar=1.0 / PIX, in1=bb_all[:, cols], op0=MULT, op1=ADD
-            )
-            nc.scalar.activation(out=gate[:, cols], in_=pooled[:, cols], func=FUNC.Sigmoid)
-        for half, part in pieces:
-            cols = columns(half, part)
-            nc.vector.scalar_tensor_tensor(
-                out=gated[:, cols], in0=gate[:, cols], scalar=1.0, in1=ft2[:, cols], op0=ADD, op1=MULT
-            )
-            nc.sync.dma_start(out=out[:, cols], in_=gated[:, cols])
+        for half, store in ((0, BANK), (1, BANK // 2)):
+            starts = range(0, BANK, PIECE)
+            for c0 in starts:
+                cols = slice(half * BANK + c0, half * BANK + c0 + PIECE)
+                nc.vector.scalar_tensor_tensor(
+                    out=pooled[:, cols], in0=pixel_sum[half][:, c0 : c0 + PIECE], scalar=1.0 / PIX, in1=bb_all[:, cols],
+                    op0=MULT, op1=ADD,
+                )
+                nc.scalar.activation(out=gate[:, cols], in_=pooled[:, cols], func=FUNC.Sigmoid)
+            for c0 in starts:
+                cols = slice(half * BANK + c0, half * BANK + c0 + PIECE)
+                nc.vector.scalar_tensor_tensor(
+                    out=gated[:, cols], in0=gate[:, cols], scalar=1.0, in1=ft2[:, cols], op0=ADD, op1=MULT
+                )
+                if (c0 + PIECE) % store == 0:
+                    done = slice(cols.stop - store, cols.stop)
+                    nc.sync.dma_start(out=out[:, done], in_=gated[:, done])

@@ -34,6 +34,7 @@ PIECE = 128
 EARLY = 6
 LOAD_PARTS = 2
 PLAIN_LAG = 2
+RIDES_LAST = 4
 LAST = 8
 EARLY_RUNS = ((0, 3), (3, 3))
 COVER_ADD = 2
@@ -270,7 +271,7 @@ def tile_joint_module_pb_kernel(tc, fv, ft, Wa_words, Wa_scales, ba, Wb_words, W
                     rhs=wb_words[:, half * 2 * BANK : (half + 1) * 2 * BANK].bitcast(FP4X4),
                     rhs_scale=wb_planes[:, half * BANK : (half + 1) * BANK],
                     start=(pix == 0),
-                    stop=(pix == PIX - 1),
+                    stop=(pix == RIDES_LAST),
                 )
 
         ftT = keep.tile([P, K_FC, 2, P], BF16)
@@ -343,7 +344,6 @@ def tile_joint_module_pb_kernel(tc, fv, ft, Wa_words, Wa_scales, ba, Wb_words, W
         multiply(1, second_wave)
         flip_late(2)
         flip_hidden(2, PAIR, "scalar", True)
-        flip_hidden(4, 1, "scalar")
         quantise_hidden(0, PAIR)
         quantise_late(2)
         multiply(2, second_wave)
@@ -352,7 +352,6 @@ def tile_joint_module_pb_kernel(tc, fv, ft, Wa_words, Wa_scales, ba, Wb_words, W
         for x0 in (5, 7):
             multiply(4, (x0, PAIR))
             multiply(5, (x0, PAIR))
-        quantise_hidden(4, 1)
         nc.vector.tensor_tensor(out=ft2[:], in0=ft2[:], in1=bfc2_all[:], op=ADD)
         add_bias(5, PAIR)
         add_bias(7, PAIR)
@@ -362,10 +361,15 @@ def tile_joint_module_pb_kernel(tc, fv, ft, Wa_words, Wa_scales, ba, Wb_words, W
         flip_hidden(5, PAIR, "vector")
         quantise_hidden(5, PAIR)
         flip_hidden(7, PAIR, "scalar")
+        flip_hidden(4, 1, "scalar")
         quantise_hidden(7, PAIR)
-        second_convolution(1, COVER_ADD, first_wave[1] - COVER_ADD)
-        second_convolution(0, COVER_ADD, PIX - COVER_ADD)
-        second_convolution(1, first_wave[1], second_wave[1])
+        quantise_hidden(4, 1)
+        second_convolution(1, COVER_ADD, 4 - COVER_ADD)
+        second_convolution(0, COVER_ADD, 4 - COVER_ADD)
+        second_convolution(0, 5, 4)
+        second_convolution(0, 4, 1)
+        second_convolution(1, 5, 4)
+        second_convolution(1, 4, 1)
 
         pooled = stream.tile([P, C_OUT], F32, tag="pooled", bufs=1)
         gate = stream.tile([P, C_OUT], F32, tag="gate", bufs=1)

@@ -66,16 +66,16 @@ def tile_joint_module_pb_kernel(tc, fv, ft, Wa_words, Wa_scales, ba, Wb_words, W
         nc.vector.memset(warm[:], 0.0)
         nc.scalar.activation(out=warm[:], in_=warm[:], func=FUNC.Sigmoid)
 
-        wa_planes = keep.tile([P, CHUNKS, HID], U8, align_bytes=64)
-        wb_planes = keep.tile([P, C_OUT], U8, align_bytes=64)
+        wa_planes = keep.tile([P, CHUNKS, HID], U8, align_bytes=256)
+        wb_planes = keep.tile([P, C_OUT], U8, align_bytes=256)
         nc.vector.memset(wa_planes[:].rearrange("p g n -> p (g n)").bitcast(I32), 0)
         nc.vector.memset(wb_planes[:].bitcast(I32), 0)
 
         fv_rows = fv.rearrange("b c i j -> b (c i j)")
         row = K_PASS * PIX
         raw = [keep.tile([P, row], BF16, name="raw%d" % g) for g in range(CHUNKS)]
-        wa_words = keep.tile([P, CHUNKS, 2 * HID], U8, align_bytes=64)
-        wb_words = keep.tile([P, 2 * C_OUT], U8, align_bytes=64)
+        wa_words = keep.tile([P, CHUNKS, 2 * HID], U8, align_bytes=256)
+        wb_words = keep.tile([P, 2 * C_OUT], U8, align_bytes=256)
         ft_sb = keep.tile([P, C_OUT], BF16)
         w_sb = keep.tile([P, HALVES, W_TILES, C_OUT], BF16)
 
@@ -115,9 +115,9 @@ def tile_joint_module_pb_kernel(tc, fv, ft, Wa_words, Wa_scales, ba, Wb_words, W
                 )
             nc.sync.dma_start(out=wb_words[:].bitcast(I32), in_=Wb_words.bitcast(I32)[0])
 
-        load_chunk(0)
         load_ft()
         load_plain_weights(0)
+        load_chunk(0)
         load_wa_scales()
         for g in range(1, CHUNKS, 2):
             load_chunk(g)
@@ -146,7 +146,7 @@ def tile_joint_module_pb_kernel(tc, fv, ft, Wa_words, Wa_scales, ba, Wb_words, W
             for x in range(n):
                 for u in range(2):
                     nc.tensor.transpose(out=bank[:, x, u, :], in_=words[:, x, u, :], identity=ident[:])
-            grouped = stream.tile([P, PAIR, P, PACK], BF16, tag="grouped", bufs=GROUPED_BUFS, align_bytes=64)
+            grouped = stream.tile([P, PAIR, P, PACK], BF16, tag="grouped", bufs=GROUPED_BUFS, align_bytes=256)
             if relu_on is None:
                 nc.scalar.copy(
                     out=grouped[:, 0:n].rearrange("p x b t -> p (x b t)").bitcast(F32)
@@ -170,10 +170,10 @@ def tile_joint_module_pb_kernel(tc, fv, ft, Wa_words, Wa_scales, ba, Wb_words, W
                 in_=grouped[:, 0:n].rearrange("p x b t -> p (x b t)"),
             )
 
-        fv_codes = keep.tile([P, CHUNKS, LAST, P], U32, align_bytes=64)
-        fv_scales = keep.tile([P, CHUNKS, LAST, P], U8, align_bytes=64)
-        last_codes = keep.tile([P, CHUNKS, P], U32, align_bytes=64)
-        last_scales = keep.tile([P, CHUNKS, P], U8, align_bytes=64)
+        fv_codes = keep.tile([P, CHUNKS, LAST, P], U32, align_bytes=256)
+        fv_scales = keep.tile([P, CHUNKS, LAST, P], U8, align_bytes=256)
+        last_codes = keep.tile([P, CHUNKS, P], U32, align_bytes=256)
+        last_scales = keep.tile([P, CHUNKS, P], U8, align_bytes=256)
         first_wave, second_wave = pixel_runs(0, PIX, SUM_BANKS)
         sorted_fv = {}
         grouped_fv = {}
@@ -241,8 +241,8 @@ def tile_joint_module_pb_kernel(tc, fv, ft, Wa_words, Wa_scales, ba, Wb_words, W
                     stop=(g == CHUNKS - 1),
                 )
 
-        h_codes = keep.tile([P, PIX, P], U32, align_bytes=64)
-        h_scales = keep.tile([P, PIX, P], U8, align_bytes=64)
+        h_codes = keep.tile([P, PIX, P], U32, align_bytes=256)
+        h_scales = keep.tile([P, PIX, P], U8, align_bytes=256)
         sorted_h = {}
         grouped_h = {}
 
@@ -310,18 +310,18 @@ def tile_joint_module_pb_kernel(tc, fv, ft, Wa_words, Wa_scales, ba, Wb_words, W
                         )
             nc.scalar.copy(out=ft2[:, cols], in_=ft2_sum[:])
 
-        sort_early(0)
-        flip_early(0)
-        quantise_early(0)
-        sort_late(0)
         flip_text_features()
         plain_layer(0)
         spread_ba()
+        sort_early(0)
+        flip_early(0)
         sort_early(1)
+        quantise_early(0)
         for g in range(1, CHUNKS):
             if g + 1 < CHUNKS:
                 sort_early(g + 1)
             else:
+                sort_late(0)
                 sort_late(1)
             flip_early(g)
             quantise_early(g)

@@ -58,6 +58,8 @@ def tile_joint_module_pb_kernel(tc, fv, ft, Wa_words, Wa_scales, ba, Wb_words, W
         ba_row = keep.tile([P, HID], BF16)
         nc.vector.memset(ba_row[:].bitcast(I32), 0)
         nc.scalar.dma_start(out=ba_row[0:1, :], in_=ba.rearrange("(o n) -> o n", o=1))
+        zeros = keep.tile([P, BANK], BF16)
+        nc.vector.memset(zeros[:].bitcast(I32), 0)
         ident = keep.tile([P, P], F32)
         make_identity(nc, ident[:])
         ones = keep.tile([P, P], BF16)
@@ -284,6 +286,11 @@ def tile_joint_module_pb_kernel(tc, fv, ft, Wa_words, Wa_scales, ba, Wb_words, W
                 nc.tensor.transpose(out=bank[:, j, :], in_=ft_sb[:].bitcast(F32)[:, j * P : (j + 1) * P], identity=ident[:])
             nc.scalar.copy(out=ftT[:], in_=bank[:].bitcast(BF16).rearrange("q j (b e) -> q j e b", e=2))
 
+        def keep_clock(count):
+            bank = flip_banks.tile([P, BANK], F32, tag="flip", name="unread")
+            for k in range(count):
+                nc.tensor.matmul(out=bank[:], lhsT=ones[:], rhs=zeros[:], start=True, stop=True)
+
         def plain_layer(half):
             cols = slice(half * BANK, (half + 1) * BANK)
             ft2_sum = sum_banks.tile([P, BANK], F32, tag="sum")
@@ -323,6 +330,8 @@ def tile_joint_module_pb_kernel(tc, fv, ft, Wa_words, Wa_scales, ba, Wb_words, W
             else:
                 sort_late(0)
                 sort_late(1)
+            if g > 1:
+                keep_clock(1)
             flip_early(g)
             quantise_early(g)
             multiply(g - 1, first_wave)

from contextlib import ExitStack

import concourse.mybir as mybir
from concourse.masks import make_identity

F32 = mybir.dt.float32
BF16 = mybir.dt.bfloat16
I32 = mybir.dt.int32
U32 = mybir.dt.uint32
U8 = mybir.dt.uint8
FP8X4 = mybir.dt.float8_e4m3fn_x4
FP4X4 = mybir.dt.float4_e2m1fn_x4
ADD = mybir.AluOpType.add
MULT = mybir.AluOpType.mult
FUNC = mybir.ActivationFunctionType

P = 128
PACK = 4
K_PASS = P * PACK
C_IN = 3072
HID = 512
C_OUT = 1024
PIX = 9
CHUNKS = C_IN // K_PASS
BANK = 512
HALVES = C_OUT // BANK
GROUPED_BUFS = 8
PAIR = 2
FLIP_BANKS = 3
SUM_BANKS = 8 - FLIP_BANKS
K_FC = C_OUT // (2 * P)
W_TILES = BANK // P
PIECE = 128
EARLY = 6
LOAD_PARTS = 2
PLAIN_LAG = 2
RIDES_LAST = 4
LAST = 8
EARLY_RUNS = ((0, 3), (3, 3))
COVER_ADD = 2

FLOPS = 2 * P * PIX * (C_IN * HID + HID * C_OUT) + 2 * P * C_OUT * C_OUT


def pixel_runs(first, count, step):
    return [(x, min(step, first + count - x)) for x in range(first, first + count, step)]


def tile_joint_module_pb_kernel(tc, fv, ft, Wa_words, Wa_scales, ba, Wb_words, Wb_scales, bb, Wfc2, bfc2, out):
    nc = tc.nc
    with ExitStack() as ctx:
        ctx.enter_context(tc.manual_schedule())
        keep = ctx.enter_context(tc.tile_pool(name="keep", bufs=1))
        stream = ctx.enter_context(tc.tile_pool(name="stream", bufs=2))
        flip_banks = ctx.enter_context(tc.psum_pool(name="flip_banks", bufs=FLIP_BANKS))
        sum_banks = ctx.enter_context(tc.psum_pool(name="sum_banks", bufs=SUM_BANKS))

        ba_row = keep.tile([P, HID], BF16)
        nc.vector.memset(ba_row[:].bitcast(I32), 0)
        nc.scalar.dma_start(out=ba_row[0:1, :], in_=ba.rearrange("(o n) -> o n", o=1))
        zeros = keep.tile([P, BANK], BF16)
        nc.vector.memset(zeros[:].bitcast(I32), 0)
        ident = keep.tile([P, P], F32)
        make_identity(nc, ident[:])
        ones = keep.tile([P, P], BF16)
        nc.vector.memset(ones[:], 1.0)
        warm = keep.tile([P, 1], F32)
        nc.vector.memset(warm[:], 0.0)
        nc.scalar.activation(out=warm[:], in_=warm[:], func=FUNC.Sigmoid)

        wa_planes = keep.tile([P, CHUNKS, HID], U8, align_bytes=256)
        wb_planes = keep.tile([P, C_OUT], U8, align_bytes=256)
        nc.vector.memset(wa_planes[:].rearrange("p g n -> p (g n)").bitcast(I32), 0)
        nc.vector.memset(wb_planes[:].bitcast(I32), 0)

        fv_rows = fv.rearrange("b c i j -> b (c i j)")
        row = K_PASS * PIX
        raw = [keep.tile([P, row], BF16, name="raw%d" % g) for g in range(CHUNKS)]
        wa_words = keep.tile([P, CHUNKS, 2 * HID], U8, align_bytes=256)
        wb_words = keep.tile([P, 2 * C_OUT], U8, align_bytes=256)
        ft_sb = keep.tile([P, C_OUT], BF16)
        w_sb = keep.tile([P, HALVES, W_TILES, C_OUT], BF16)

        def load_chunk(g):
            piece = row // LOAD_PARTS
            for k in range(LOAD_PARTS):
                nc.sync.dma_start(
                    out=raw[g][:, k * piece : (k + 1) * piece],
                    in_=fv_rows[:, g * row + k * piece : g * row + (k + 1) * piece],
                )

        w_rows = Wfc2.rearrange("(h r a) c -> h r a c", r=P, a=W_TILES)

        def load_plain_weights(half):
            nc.sync.dma_start(out=w_sb[:, half], in_=w_rows[half])

        def load_ft():
            nc.sync.dma_start(out=ft_sb[:], in_=ft)

        def load_wa_scales():
            for quad in range(4):
                nc.sync.dma_start(
                    out=wa_planes[32 * quad : 32 * quad + 4].bitcast(I32),
                    in_=Wa_scales.bitcast(I32)[:, 4 * quad : 4 * quad + 4, :].rearrange("g r n -> r g n"),
                )

        def load_wa_words(g0=0, g1=CHUNKS):
            nc.sync.dma_start(
                out=wa_words[:, g0:g1, :].bitcast(I32), in_=Wa_words.bitcast(I32)[g0:g1].rearrange("g p n -> p g n")
            )

        def load_wb():
            for quad in range(4):
                nc.sync.dma_start(
                    out=wb_planes[32 * quad : 32 * quad + 4].bitcast(I32),
                    in_=Wb_scales.bitcast(I32)[0, 4 * quad : 4 * quad + 4, :],
                )
            nc.sync.dma_start(out=wb_words[:].bitcast(I32), in_=Wb_words.bitcast(I32)[0])

        load_ft()
        load_plain_weights(0)
        load_chunk(0)
        load_wa_scales()
        for g in range(1, CHUNKS, 2):
            load_chunk(g)
            load_wa_words(g - 1, g + 1)
            if g + 1 < CHUNKS:
                load_chunk(g + 1)
        load_plain_weights(1)
        load_wb()
        bb_all = keep.tile([P, C_OUT], BF16)
        bfc2_all = keep.tile([P, C_OUT], BF16)
        nc.sync.dma_start(out=bb_all[:], in_=bb.partition_broadcast(P))
        nc.sync.dma_start(out=bfc2_all[:], in_=bfc2.partition_broadcast(P))

        ba_all = keep.tile([P, HID], F32)

        def spread_ba():
            spread = sum_banks.tile([P, BANK], F32, tag="sum")
            nc.tensor.matmul(out=spread[:], lhsT=ones[:], rhs=ba_row[:], start=True, stop=True)
            nc.scalar.copy(out=ba_all[:], in_=spread[:])

        def flip(words, n, relu_on, spare=False):
            if spare:
                bank = sum_banks.tile([P, PAIR, 2, P], F32, tag="sum")
            else:
                bank = flip_banks.tile([P, PAIR, 2, P], F32, tag="flip")
            for x in range(n):
                for u in range(2):
                    nc.tensor.transpose(out=bank[:, x, u, :], in_=words[:, x, u, :], identity=ident[:])
            grouped = stream.tile([P, PAIR, P, PACK], BF16, tag="grouped", bufs=GROUPED_BUFS, align_bytes=256)
            if relu_on is None:
                nc.scalar.copy(
                    out=grouped[:, 0:n].rearrange("p x b t -> p (x b t)").bitcast(F32)
                    .rearrange("p (x b u) -> p x b u", x=n, u=2),
                    in_=bank[:, 0:n].rearrange("p x u b -> p x b u"),
                )
            else:
                for x in range(n):
                    h_out = grouped[:, x].rearrange("p b (u e) -> p b u e", u=2)
                    h_in = bank[:, x].bitcast(BF16).rearrange("p u (b e) -> p b u e", e=2)
                    if relu_on == "vector":
                        nc.vector.tensor_scalar_max(out=h_out, in0=h_in, scalar1=0.0)
                    else:
                        nc.scalar.activation(out=h_out, in_=h_in, func=FUNC.Relu)
            return grouped

        def quantise(grouped, n, codes, scales):
            nc.vector.quantize_mx(
                out=codes.rearrange("p x b -> p (x b)").bitcast(FP8X4),
                scales=scales.rearrange("p x b -> p (x b)"),
                in_=grouped[:, 0:n].rearrange("p x b t -> p (x b t)"),
            )

        fv_codes = keep.tile([P, CHUNKS, LAST, P], U32, align_bytes=256)
        fv_scales = keep.tile([P, CHUNKS, LAST, P], U8, align_bytes=256)
        last_codes = keep.tile([P, CHUNKS, P], U32, align_bytes=256)
        last_scales = keep.tile([P, CHUNKS, P], U8, align_bytes=256)
        first_wave, second_wave = pixel_runs(0, PIX, SUM_BANKS)
        sorted_fv = {}
        grouped_fv = {}
        hidden = {}

        def sort_pixels(out, g, x0, n, rows=slice(0, P)):
            nc.vector.tensor_copy(
                out=out[:, :, :, rows, :].rearrange("b x u p e -> b u p e x"),
                in_=raw[g][:].rearrange("b (p u e x) -> b u p e x", u=2, e=2, x=PIX)[:, :, rows, :, x0 : x0 + n],
            )

        def as_words(tile_x):
            return tile_x.rearrange("b x u p e -> b x u (p e)").bitcast(F32)

        def sort_early(g):
            sorted_fv[g] = stream.tile([P, EARLY, 2, P, 2], BF16, tag="sorted", bufs=3, name="sorted")
            for k in range(LOAD_PARTS):
                rows = slice(k * P // LOAD_PARTS, (k + 1) * P // LOAD_PARTS)
                for x0, n in EARLY_RUNS:
                    sort_pixels(sorted_fv[g][:, x0 : x0 + n], g, x0, n, rows)

        def flip_early(g):
            words = as_words(sorted_fv[g][:])
            grouped_fv[g] = [flip(words[:, x0 : x0 + PAIR], PAIR, None) for x0 in range(0, EARLY, PAIR)]

        def quantise_early(g):
            for grouped, x0 in zip(grouped_fv[g], range(0, EARLY, PAIR)):
                quantise(grouped, PAIR, fv_codes[:, g, x0 : x0 + PAIR, :], fv_scales[:, g, x0 : x0 + PAIR, :])

        def sort_late(g):
            k = g // 2
            if g % 2 == 0:
                sorted_fv["late", k] = stream.tile([P, 2, 3, 2, P, 2], BF16, tag="sorted_late", bufs=2, name="sorted_late")
            sort_pixels(sorted_fv["late", k][:, g % 2], g, EARLY, 3)

        def flip_late(k):
            both = sorted_fv["late", k]
            words = both[:].rearrange("b s x u p e -> b s x u (p e)").bitcast(F32)
            grouped_fv["late", k] = [
                flip(words[:, 0, 0:PAIR], PAIR, None), flip(words[:, :, PAIR], 2, None), flip(words[:, 1, 0:PAIR], PAIR, None)
            ]

        def quantise_late(k):
            g = 2 * k
            one, last, two = grouped_fv["late", k]
            quantise(one, PAIR, fv_codes[:, g, EARLY:LAST, :], fv_scales[:, g, EARLY:LAST, :])
            quantise(last, 2, last_codes[:, g : g + 2, :], last_scales[:, g : g + 2, :])
            quantise(two, PAIR, fv_codes[:, g + 1, EARLY:LAST, :], fv_scales[:, g + 1, EARLY:LAST, :])

        def multiply(g, wave):
            first, count = wave
            for pix in range(first, first + count):
                if g == 0:
                    hidden[pix] = sum_banks.tile([P, HID], F32, tag="sum", name="hidden")
                codes, scales = (last_codes[:, g, :], last_scales[:, g, :]) if pix == LAST else (
                    fv_codes[:, g, pix, :], fv_scales[:, g, pix, :]
                )
                nc.tensor.matmul_mx(
                    out=hidden[pix][:],
                    lhsT=codes.bitcast(FP8X4),
                    lhsT_scale=scales,
                    rhs=wa_words[:, g, :].bitcast(FP4X4),
                    rhs_scale=wa_planes[:, g, :],
                    start=(g == 0),
                    stop=(g == CHUNKS - 1),
                )

        h_codes = keep.tile([P, PIX, P], U32, align_bytes=256)
        h_scales = keep.tile([P, PIX, P], U8, align_bytes=256)
        sorted_h = {}
        grouped_h = {}

        def add_bias(x0, n):
            sorted_h[x0] = stream.tile([P, PAIR, 2, P, 2], BF16, tag="sorted_h", bufs=4, name="sorted_h")
            for x in range(n):
                nc.vector.tensor_tensor(
                    out=sorted_h[x0][:, x],
                    in0=hidden[x0 + x][:].rearrange("b (p u e) -> b u p e", u=2, e=2),
                    in1=ba_all[:].rearrange("b (p u e) -> b u p e", u=2, e=2),
                    op=ADD,
                )

        def flip_hidden(x0, n, relu_on, spare=False):
            grouped_h[x0] = flip(as_words(sorted_h[x0][:]), n, relu_on, spare)

        def quantise_hidden(x0, n):
            quantise(grouped_h[x0], n, h_codes[:, x0 : x0 + n, :], h_scales[:, x0 : x0 + n, :])

        def second_convolution(half, first, count):
            for pix in range(first, first + count):
                nc.tensor.matmul_mx(
                    out=pixel_sum[half][:],
                    lhsT=h_codes[:, pix, :].bitcast(FP8X4),
                    lhsT_scale=h_scales[:, pix, :],
                    rhs=wb_words[:, half * 2 * BANK : (half + 1) * 2 * BANK].bitcast(FP4X4),
                    rhs_scale=wb_planes[:, half * BANK : (half + 1) * BANK],
                    start=(pix == 0),
                    stop=(pix == RIDES_LAST),
                )

        ftT = keep.tile([P, K_FC, 2, P], BF16)
        wT = keep.tile([P, K_FC, C_OUT, 2], BF16)
        ft2 = keep.tile([P, C_OUT], F32)

        def flip_text_features():
            bank = flip_banks.tile([P, K_FC, P], F32, tag="flip")
            for j in range(K_FC):
                nc.tensor.transpose(out=bank[:, j, :], in_=ft_sb[:].bitcast(F32)[:, j * P : (j + 1) * P], identity=ident[:])
            nc.scalar.copy(out=ftT[:], in_=bank[:].bitcast(BF16).rearrange("q j (b e) -> q j e b", e=2))

        def keep_clock(count):
            bank = flip_banks.tile([P, BANK], F32, tag="flip", name="unread")
            for k in range(count):
                nc.tensor.matmul(out=bank[:], lhsT=ones[:], rhs=zeros[:], start=True, stop=True)

        def plain_layer(half):
            cols = slice(half * BANK, (half + 1) * BANK)
            ft2_sum = sum_banks.tile([P, BANK], F32, tag="sum")
            for j in range(K_FC + PLAIN_LAG):
                if j < K_FC:
                    bank = flip_banks.tile([P, W_TILES, P], F32, tag="flip")
                    for a in range(W_TILES):
                        nc.tensor.transpose(
                            out=bank[:, a, :],
                            in_=w_sb[:, half, a, :].bitcast(F32)[:, j * P : (j + 1) * P],
                            identity=ident[:],
                        )
                    nc.scalar.copy(
                        out=wT[:, j, cols, :].rearrange("q o e -> q (o e)").bitcast(F32)
                        .rearrange("q (r a) -> q r a", a=W_TILES),
                        in_=bank[:].rearrange("q a r -> q r a"),
                    )
                if j >= PLAIN_LAG:
                    i = j - PLAIN_LAG
                    for e in range(2):
                        nc.tensor.matmul(
                            out=ft2_sum[:], lhsT=ftT[:, i, e, :], rhs=wT[:, i, cols, e],
                            start=(i == 0 and e == 0), stop=(i == K_FC - 1 and e == 1),
                        )
            nc.scalar.copy(out=ft2[:, cols], in_=ft2_sum[:])

        flip_text_features()
        plain_layer(0)
        spread_ba()
        sort_early(0)
        flip_early(0)
        sort_early(1)
        quantise_early(0)
        for g in range(1, CHUNKS):
            if g + 1 < CHUNKS:
                sort_early(g + 1)
            else:
                sort_late(0)
                sort_late(1)
            if g > 1:
                keep_clock(1)
            flip_early(g)
            quantise_early(g)
            multiply(g - 1, first_wave)
        flip_late(0)
        quantise_late(0)
        multiply(CHUNKS - 1, first_wave)
        add_bias(0, PAIR)
        sort_late(2)
        add_bias(2, PAIR)
        sort_late(3)
        add_bias(4, 1)
        plain_layer(1)
        flip_late(1)
        flip_hidden(0, PAIR, "scalar", True)
        sort_late(4)
        quantise_late(1)
        sort_late(5)
        multiply(0, second_wave)
        multiply(1, second_wave)
        flip_late(2)
        flip_hidden(2, PAIR, "scalar", True)
        quantise_hidden(0, PAIR)
        quantise_late(2)
        multiply(2, second_wave)
        multiply(3, second_wave)
        quantise_hidden(2, PAIR)
        for x0 in (5, 7):
            multiply(4, (x0, PAIR))
            multiply(5, (x0, PAIR))
        nc.vector.tensor_tensor(out=ft2[:], in0=ft2[:], in1=bfc2_all[:], op=ADD)
        add_bias(5, PAIR)
        add_bias(7, PAIR)
        pixel_sum = [sum_banks.tile([P, BANK], F32, tag="sum", name="pixel_sum") for half in range(HALVES)]
        for half in range(HALVES):
            second_convolution(half, 0, COVER_ADD)
        flip_hidden(5, PAIR, "vector")
        quantise_hidden(5, PAIR)
        flip_hidden(7, PAIR, "scalar")
        flip_hidden(4, 1, "scalar")
        quantise_hidden(7, PAIR)
        quantise_hidden(4, 1)
        second_convolution(1, COVER_ADD, 4 - COVER_ADD)
        second_convolution(0, COVER_ADD, 4 - COVER_ADD)
        second_convolution(0, 5, 4)
        second_convolution(0, 4, 1)
        second_convolution(1, 5, 4)
        second_convolution(1, 4, 1)

        pooled = stream.tile([P, C_OUT], F32, tag="pooled", bufs=1)
        gate = stream.tile([P, C_OUT], F32, tag="gate", bufs=1)
        gated = stream.tile([P, C_OUT], F32, tag="gated", bufs=1)
        for half, store in ((0, BANK), (1, BANK // 2)):
            starts = range(0, BANK, PIECE)
            for c0 in starts:
                cols = slice(half * BANK + c0, half * BANK + c0 + PIECE)
                nc.vector.scalar_tensor_tensor(
                    out=pooled[:, cols], in0=pixel_sum[half][:, c0 : c0 + PIECE], scalar=1.0 / PIX, in1=bb_all[:, cols],
                    op0=MULT, op1=ADD,
                )
                nc.scalar.activation(out=gate[:, cols], in_=pooled[:, cols], func=FUNC.Sigmoid)
            for c0 in starts:
                cols = slice(half * BANK + c0, half * BANK + c0 + PIECE)
                nc.vector.scalar_tensor_tensor(
                    out=gated[:, cols], in0=gate[:, cols], scalar=1.0, in1=ft2[:, cols], op0=ADD, op1=MULT
                )
                if (c0 + PIECE) % store == 0:
                    done = slice(cols.stop - store, cols.stop)
                    nc.sync.dma_start(out=out[:, done], in_=gated[:, done])
